import numpy as np
import ml_dtypes


def mxq(x, axis, fmt="e4m3"):
    dtype, down = {"e4m3": (ml_dtypes.float8_e4m3fn, 7), "e5m2": (ml_dtypes.float8_e5m2, 14)}[fmt]
    v = np.moveaxis(np.asarray(x, np.float32).astype(ml_dtypes.bfloat16).astype(np.float64), axis, -1)
    blocks = v.reshape(v.shape[:-1] + (-1, 32))
    amax = np.abs(blocks).max(-1, keepdims=True)
    byte = np.maximum(np.where(amax > 0, np.frexp(amax)[1] - 1 + 127, 0) - down, 1)
    scale = np.exp2(byte - 127.0)
    codes = (blocks / scale).astype(np.float32).astype(dtype).astype(np.float64)
    return np.moveaxis((codes * scale).reshape(v.shape), -1, axis)


WIDE = False


def mx_kscale(k, group=512):
    if not WIDE:
        return np.ones(k)
    levels = np.array([10, -10, 5, -5, 0])
    if group != 512:
        return np.exp2(np.random.permutation(np.resize(levels, k // group))).repeat(group)
    a = np.random.permutation(np.resize(levels, k // 512 * 4)).reshape(k // 512, 4)
    idx = np.arange(k)
    return np.exp2(a[idx // 512, idx % 128 // 32])


BF16 = ml_dtypes.bfloat16


def bf(x):
    return np.asarray(x, np.float32).astype(BF16)


def f64(x):
    return np.asarray(x).astype(np.float64)


B, T, N, M, D, F = 2, 2, 32, 32, 512, 512
K = 4 * D


def silu(x):
    return x / (1.0 + np.exp(-x))


def setup_inputs():
    s = mx_kscale(D, D)
    u = np.concatenate([s, s, s * s, s])
    return {
        "p": bf(np.random.standard_normal((B, T, N, D)) * s),
        "v": bf(np.random.standard_normal((B, T, M, D)) * s),
        "W1": bf(np.random.standard_normal((K, F)) * 0.9 / np.sqrt(K) / u[:, None]),
        "b1": bf(np.random.standard_normal(F) * 0.3),
        "W2": bf(np.random.standard_normal((F, D)) * 1.5 / np.sqrt(F)),
        "b2": bf(np.random.standard_normal(D) * 0.3),
    }


def reference(p, v, W1, b1, W2, b2):
    p4 = f64(p)[:, :, :, None, :]
    v4 = f64(v)[:, :, None, :, :]
    prod = p4 * v4
    absdiff = np.abs(p4 - v4)
    full = prod.shape
    pair = np.concatenate([np.broadcast_to(p4, full), np.broadcast_to(v4, full), prod, absdiff], axis=-1)
    h = silu((mxq(pair, 4, "e4m3") @ mxq(f64(W1), 0, "e4m3")) + f64(b1))
    grid = (mxq(h, 4, "e4m3") @ mxq(f64(W2), 0, "e4m3")) + f64(b2)
    return grid.reshape(B, T, N * M, D)

@@ -1,0 +1,319 @@
+from contextlib import ExitStack
+
+import concourse.mybir as mybir
+from concourse.masks import make_identity
+
+BF16 = mybir.dt.bfloat16
+F32 = mybir.dt.float32
+I32 = mybir.dt.int32
+U32 = mybir.dt.uint32
+U8 = mybir.dt.uint8
+FP8X4 = mybir.dt.float8_e4m3fn_x4
+ACT = mybir.ActivationFunctionType
+ALU = mybir.AluOpType
+
+P = 128
+PACK = 4
+K_PASS = P * PACK
+STEPS = 4
+POINTS = 32
+D = 512
+F = 512
+TILE_ROWS = 512
+TILE_POINTS = TILE_ROWS // POINTS
+TILES = STEPS * POINTS * POINTS // TILE_ROWS
+QUARTERS = 4
+UNITS = TILES * QUARTERS
+WEIGHT_CHUNKS = 5
+W2_CHUNK = 4
+
+DIFFERENCE_LEAD = 7
+PRODUCT_LEAD = 6
+HIDDEN_LAG = 4
+LAYER2_LAG = 6
+STORE_LAG = 7
+
+HIDDEN_ROWS_ON_VECTOR = 256
+
+FLOPS = 2 * STEPS * POINTS * POINTS * (4 * D * F + F * D)
+
+
+def tile_pairinteractiongrid_pa_kernel(tc, p, v, W1, b1, W2, b2, out):
+    nc = tc.nc
+    p_rows = p.flatten_outer_dims()
+    v_rows = v.flatten_outer_dims()
+    out_rows = out.flatten_outer_dims()
+
+    with ExitStack() as stack:
+        consts = stack.enter_context(tc.tile_pool(name="consts", bufs=1))
+        weights = stack.enter_context(tc.tile_pool(name="weights", bufs=3))
+        pairs = stack.enter_context(tc.tile_pool(name="pairs", bufs=2))
+        hidden = stack.enter_context(tc.tile_pool(name="hidden", bufs=2))
+        results = stack.enter_context(tc.tile_pool(name="results", bufs=6))
+        psum = stack.enter_context(tc.psum_pool(name="psum", bufs=2))
+
+        inputs_by_row = consts.tile([P, 2, D], BF16)
+        nc.sync.dma_start(out=inputs_by_row[0:64, :, :], in_=p_rows.rearrange("(h r) d -> r h d", h=2))
+        nc.sync.dma_start(out=inputs_by_row[64:128, :, :], in_=v_rows.rearrange("(h r) d -> r h d", h=2))
+        b1_rows = consts.tile([P, P], BF16)
+        nc.gpsimd.memset(b1_rows[:], 0.0)
+        nc.sync.dma_start(out=b1_rows[0:PACK, :], in_=b1.rearrange("(t q) -> t q", q=P))
+        weight_raw = []
+        for w in range(WEIGHT_CHUNKS):
+            rows = W2 if w == W2_CHUNK else W1[w * K_PASS : (w + 1) * K_PASS, :]
+            raw = weights.tile([P, PACK, F], BF16, bufs=WEIGHT_CHUNKS)
+            nc.sync.dma_start(out=raw[:], in_=rows.rearrange("(t q) f -> q t f", q=P))
+            weight_raw.append(raw)
+        b2_everywhere = consts.tile([P, D], BF16)
+        nc.sync.dma_start(out=b2_everywhere[:], in_=b2.partition_broadcast(P))
+
+        zero_column = consts.tile([P, 1], F32)
+        nc.vector.memset(zero_column[:], 0.0)
+        warm_column = consts.tile([P, 1], F32)
+        nc.scalar.activation(out=warm_column[:], in_=zero_column[:], func=ACT.Silu)
+
+        identity = consts.tile([P, P], BF16)
+        make_identity(nc, identity[:])
+        chooser = consts.tile([P, 2, POINTS, POINTS], BF16)
+        for e in range(2):
+            nc.vector.tensor_tensor(
+                out=chooser[:, e, :, :],
+                in0=identity[:, POINTS * e : POINTS * (e + 1)].unsqueeze(2).to_broadcast([P, POINTS, POINTS]),
+                in1=identity[:, 64 + POINTS * e : 64 + POINTS * (e + 1)].unsqueeze(1).to_broadcast([P, POINTS, POINTS]),
+                op=ALU.subtract,
+            )
+
+        transposed = psum.tile([P, 2, PACK, P], BF16, tag="layer2")
+        for h in range(2):
+            for t in range(PACK):
+                nc.tensor.transpose(transposed[:, h, t, :], inputs_by_row[:, h, t * P : (t + 1) * P], identity[:])
+        b1_transposed = psum.tile([P, P], BF16, tag="difference")
+        nc.tensor.transpose(b1_transposed[:], b1_rows[:], identity[:])
+        p_by_k = consts.tile([P, P, PACK], BF16, align_bytes=64)
+        v_by_k = consts.tile([P, P, PACK], BF16, align_bytes=64)
+        nc.vector.tensor_copy(
+            out=p_by_k[:].rearrange("q (h r) t -> q h r t", h=2),
+            in_=transposed[:, :, :, 0:64].rearrange("q h t r -> q h r t"),
+        )
+        nc.vector.tensor_copy(
+            out=v_by_k[:].rearrange("q (h r) t -> q h r t", h=2),
+            in_=transposed[:, :, :, 64:128].rearrange("q h t r -> q h r t"),
+        )
+        b1_by_group = consts.tile([P, QUARTERS], F32)
+        nc.vector.tensor_copy(out=b1_by_group[:], in_=b1_transposed[:, 0:QUARTERS])
+
+        p_fourfold = consts.tile([P, P, 4, PACK], BF16, align_bytes=64)
+        nc.vector.tensor_copy(out=p_fourfold[:], in_=p_by_k[:].unsqueeze(2).to_broadcast([P, P, 4, PACK]))
+        p_codes = consts.tile([P, P * 4], U32, align_bytes=64)
+        p_scales = consts.tile([P, P * 4], U8, align_bytes=64)
+        v_codes = consts.tile([P, P], U32, align_bytes=64)
+        v_scales = consts.tile([P, P], U8, align_bytes=64)
+        nc.vector.memset(p_scales[:].bitcast(I32), 0)
+        nc.vector.memset(v_scales[:].bitcast(I32), 0)
+        nc.vector.quantize_mx(
+            out=v_codes[:].bitcast(FP8X4), scales=v_scales[:], in_=v_by_k[:].rearrange("q r t -> q (r t)")
+        )
+        nc.vector.quantize_mx(
+            out=p_codes[:].bitcast(FP8X4), scales=p_scales[:], in_=p_fourfold[:].rearrange("q r c t -> q (r c t)")
+        )
+
+        weight_codes = consts.tile([P, WEIGHT_CHUNKS, F], U32, align_bytes=64)
+        weight_scales = consts.tile([P, WEIGHT_CHUNKS, F], U8, align_bytes=64)
+        weight_grouped = {}
+
+        def regroup(copy, grouped, planes):
+            copy(
+                out=grouped.rearrange("q (c i) t -> q c t i", i=4),
+                in_=planes.rearrange("q t (c i) -> q c t i", i=4),
+            )
+
+        def regroup_weight(w):
+            grouped = weights.tile([P, F, PACK], BF16, align_bytes=64)
+            regroup(nc.vector.tensor_copy if w % 2 == 0 else nc.scalar.copy, grouped[:], weight_raw[w][:])
+            weight_grouped[w] = grouped
+
+        def quantise_weight(w):
+            nc.vector.quantize_mx(
+                out=weight_codes[:, w, :].bitcast(FP8X4),
+                scales=weight_scales[:, w, :],
+                in_=weight_grouped[w][:].rearrange("q f t -> q (f t)"),
+            )
+
+        p_part = {}
+        v_part = {}
+        product_part = {}
+        difference_part = {}
+        product_values = {}
+        difference_values = {}
+        hidden_planes = {}
+        hidden_grouped = {}
+        hidden_part = {}
+        layer2_banks = {}
+
+        def difference_slice(unit):
+            i, u = divmod(unit, QUARTERS)
+            step, half = divmod(i, 2)
+            h, e = divmod(step, 2)
+            if u == 0:
+                values = pairs.tile([P, TILE_ROWS, PACK], BF16, align_bytes=64, name="difference_values")
+                difference_values[i] = values
+            first_point = TILE_POINTS * half + 4 * u
+            bank = psum.tile([P, PACK, P], F32, tag="difference")
+            for t in range(PACK):
+                nc.tensor.matmul(
+                    out=bank[:, t, :],
+                    lhsT=inputs_by_row[:, h, t * P : (t + 1) * P],
+                    rhs=chooser[:, e, first_point : first_point + 4, :].rearrange("k n m -> k (n m)"),
+                    start=True,
+                    stop=True,
+                )
+            nc.scalar.activation(
+                out=difference_values[i][:, u * P : (u + 1) * P, :],
+                in_=bank[:].rearrange("q t r -> q r t"),
+                func=ACT.Abs,
+            )
+
+        def quantise(values, name):
+            codes = pairs.tile([P, TILE_ROWS], U32, align_bytes=64, name=name + "_codes", bufs=3)
+            scales = pairs.tile([P, TILE_ROWS], U8, align_bytes=64, name=name + "_scales", bufs=3)
+            nc.vector.quantize_mx(out=codes[:].bitcast(FP8X4), scales=scales[:], in_=values)
+            return codes, scales
+
+        def multiply(i):
+            step = i // 2
+            values = pairs.tile([P, TILE_POINTS, POINTS, PACK], BF16, align_bytes=64, name="product_values")
+            shape = [P, TILE_POINTS, POINTS, PACK]
+            nc.vector.tensor_tensor(
+                out=values[:],
+                in0=p_by_k[:, TILE_POINTS * i : TILE_POINTS * (i + 1), :].unsqueeze(2).to_broadcast(shape),
+                in1=v_by_k[:, POINTS * step : POINTS * (step + 1), :].unsqueeze(1).to_broadcast(shape),
+                op=ALU.mult,
+            )
+            product_values[i] = values
+
+        def spread_p_and_v(i):
+            step, half = divmod(i, 2)
+            codes = pairs.tile([P, TILE_ROWS], U32, align_bytes=64, name="p_part_codes", bufs=3)
+            scales = pairs.tile([P, TILE_ROWS], U8, align_bytes=64, name="p_part_scales", bufs=3)
+            first = 4 * TILE_POINTS * i
+            nc.vector.tensor_copy(
+                out=codes[:].bitcast(I32).rearrange("q (n r c) -> q n r c", r=8, c=4),
+                in_=p_codes[:, first : first + 4 * TILE_POINTS]
+                .bitcast(I32)
+                .rearrange("q (n c) -> q n c", c=4)
+                .unsqueeze(2)
+                .to_broadcast([P, TILE_POINTS, 8, 4]),
+            )
+            nc.vector.tensor_copy(
+                out=scales[:].bitcast(I32).rearrange("q (n r) -> q n r", r=8),
+                in_=p_scales[:, first : first + 4 * TILE_POINTS].bitcast(I32).unsqueeze(2).to_broadcast([P, TILE_POINTS, 8]),
+            )
+            p_part[i] = (codes, scales)
+            if half == 1:
+                v_part[i] = v_part[i - 1]
+                return
+            codes = pairs.tile([P, TILE_ROWS], U32, align_bytes=64, name="v_part_codes")
+            scales = pairs.tile([P, TILE_ROWS], U8, align_bytes=64, name="v_part_scales")
+            nc.vector.tensor_copy(
+                out=codes[:].bitcast(I32).rearrange("q (n m) -> q n m", m=POINTS),
+                in_=v_codes[:, POINTS * step : POINTS * (step + 1)].bitcast(I32).unsqueeze(1).to_broadcast([P, TILE_POINTS, POINTS]),
+            )
+            nc.vector.tensor_copy(
+                out=scales[:].bitcast(I32).rearrange("q (n c) -> q n c", c=POINTS // 4),
+                in_=v_scales[:, POINTS * step : POINTS * (step + 1)].bitcast(I32).unsqueeze(1).to_broadcast([P, TILE_POINTS, POINTS // 4]),
+            )
+            v_part[i] = (codes, scales)
+
+        def layer1_group(unit):
+            i, j = divmod(unit, QUARTERS)
+            if j == 0:
+                planes = hidden.tile([P, QUARTERS, TILE_ROWS], BF16, name="hidden_planes")
+                hidden_planes[i] = planes
+            bank = psum.tile([P, TILE_ROWS], F32, tag="layer1", bufs=4)
+            parts = [p_part[i], v_part[i], product_part[i], difference_part[i]]
+            for w, (codes, scales) in enumerate(parts):
+                nc.tensor.matmul_mx(
+                    out=bank[:],
+                    lhsT=weight_codes[:, w, j * P : (j + 1) * P].bitcast(FP8X4),
+                    lhsT_scale=weight_scales[:, w, j * P : (j + 1) * P],
+                    rhs=codes[:].bitcast(FP8X4),
+                    rhs_scale=scales[:],
+                    start=(w == 0),
+                    stop=(w == len(parts) - 1),
+                )
+            nc.scalar.activation(
+                out=hidden_planes[i][:, j, :], in_=bank[:], func=ACT.Silu, bias=b1_by_group[:, j : j + 1]
+            )
+
+        def regroup_hidden(i):
+            grouped = hidden.tile([P, TILE_ROWS, PACK], BF16, align_bytes=64, name="hidden_grouped")
+            cut = HIDDEN_ROWS_ON_VECTOR
+            regroup(nc.vector.tensor_copy, grouped[:, 0:cut, :], hidden_planes[i][:, :, 0:cut])
+            regroup(nc.scalar.copy, grouped[:, cut:TILE_ROWS, :], hidden_planes[i][:, :, cut:TILE_ROWS])
+            hidden_grouped[i] = grouped
+
+        def quantise_hidden(i):
+            codes = hidden.tile([P, TILE_ROWS], U32, align_bytes=64, name="hidden_codes")
+            scales = hidden.tile([P, TILE_ROWS], U8, align_bytes=64, name="hidden_scales")
+            nc.vector.quantize_mx(
+                out=codes[:].bitcast(FP8X4), scales=scales[:], in_=hidden_grouped[i][:].rearrange("q r t -> q (r t)")
+            )
+            hidden_part[i] = (codes, scales)
+
+        def layer2_slice(unit):
+            i, u = divmod(unit, QUARTERS)
+            codes, scales = hidden_part[i]
+            bank = psum.tile([P, D], F32, tag="layer2")
+            nc.tensor.matmul_mx(
+                out=bank[:],
+                lhsT=codes[:, u * P : (u + 1) * P].bitcast(FP8X4),
+                lhsT_scale=scales[:, u * P : (u + 1) * P],
+                rhs=weight_codes[:, W2_CHUNK, :].bitcast(FP8X4),
+                rhs_scale=weight_scales[:, W2_CHUNK, :],
+                start=True,
+                stop=True,
+            )
+            layer2_banks[unit] = bank
+
+        def add_bias_and_store(unit):
+            result = results.tile([P, D], F32)
+            nc.vector.tensor_tensor(out=result[:], in0=layer2_banks[unit][:], in1=b2_everywhere[:], op=ALU.add)
+            nc.sync.dma_start(out=out_rows[unit * P : (unit + 1) * P, :], in_=result[:])
+
+        def tile_starting_at(slot):
+            i, j = divmod(slot, QUARTERS)
+            return i if j == 0 and 0 <= i < TILES else None
+
+        for slot in range(-DIFFERENCE_LEAD, UNITS + STORE_LAG):
+            w = slot + DIFFERENCE_LEAD
+            if w < WEIGHT_CHUNKS:
+                regroup_weight(w)
+            if 1 <= w <= WEIGHT_CHUNKS:
+                quantise_weight(w - 1)
+
+            if 0 <= slot - STORE_LAG:
+                add_bias_and_store(slot - STORE_LAG)
+            if slot + DIFFERENCE_LEAD < UNITS:
+                difference_slice(slot + DIFFERENCE_LEAD)
+
+            i = tile_starting_at(slot + PRODUCT_LEAD)
+            if i is not None:
+                multiply(i)
+            i = tile_starting_at(slot + PRODUCT_LEAD - 1)
+            if i is not None:
+                spread_p_and_v(i)
+                product_part[i] = quantise(product_values[i][:].rearrange("q n m t -> q (n m t)"), "product")
+            i = tile_starting_at(slot + DIFFERENCE_LEAD - QUARTERS)
+            if i is not None:
+                difference_part[i] = quantise(difference_values[i][:].rearrange("q r t -> q (r t)"), "difference")
+            i = tile_starting_at(slot - HIDDEN_LAG)
+            if i is not None:
+                regroup_hidden(i)
+            i = tile_starting_at(slot - HIDDEN_LAG - 1)
+            if i is not None:
+                quantise_hidden(i)
+
+            if 0 <= slot < UNITS:
+                layer1_group(slot)
+            if 0 <= slot - LAYER2_LAG < UNITS:
+                layer2_slice(slot - LAYER2_LAG)

@@ -24,11 +24,13 @@ TILE_POINTS = TILE_ROWS // POINTS
 TILES = STEPS * POINTS * POINTS // TILE_ROWS
 QUARTERS = 4
 UNITS = TILES * QUARTERS
-WEIGHT_CHUNKS = 5
-W2_CHUNK = 4
+PARTS = 4
+W2_PIECE = 4
 
+INPUT_LEAD = 7
 DIFFERENCE_LEAD = 7
 PRODUCT_LEAD = 6
+WEIGHT_LEAD = 2
 HIDDEN_LAG = 4
 LAYER2_LAG = 6
 STORE_LAG = 7
@@ -51,6 +53,7 @@ def tile_pairinteractiongrid_pa_kernel(tc, p, v, W1, b1, W2, b2, out):
         hidden = stack.enter_context(tc.tile_pool(name="hidden", bufs=2))
         results = stack.enter_context(tc.tile_pool(name="results", bufs=6))
         psum = stack.enter_context(tc.psum_pool(name="psum", bufs=2))
+        stack.enter_context(tc.manual_schedule())
 
         inputs_by_row = consts.tile([P, 2, D], BF16)
         nc.sync.dma_start(out=inputs_by_row[0:64, :, :], in_=p_rows.rearrange("(h r) d -> r h d", h=2))
@@ -59,9 +62,9 @@ def tile_pairinteractiongrid_pa_kernel(tc, p, v, W1, b1, W2, b2, out):
         nc.gpsimd.memset(b1_rows[:], 0.0)
         nc.sync.dma_start(out=b1_rows[0:PACK, :], in_=b1.rearrange("(t q) -> t q", q=P))
         weight_raw = []
-        for w in range(WEIGHT_CHUNKS):
-            rows = W2 if w == W2_CHUNK else W1[w * K_PASS : (w + 1) * K_PASS, :]
-            raw = weights.tile([P, PACK, F], BF16, bufs=WEIGHT_CHUNKS)
+        for c in range(PARTS + 1):
+            rows = W2 if c == PARTS else W1[c * K_PASS : (c + 1) * K_PASS, :]
+            raw = weights.tile([P, PACK, F], BF16, bufs=PARTS + 1)
             nc.sync.dma_start(out=raw[:], in_=rows.rearrange("(t q) f -> q t f", q=P))
             weight_raw.append(raw)
         b2_everywhere = consts.tile([P, D], BF16)
@@ -71,6 +74,13 @@ def tile_pairinteractiongrid_pa_kernel(tc, p, v, W1, b1, W2, b2, out):
         nc.vector.memset(zero_column[:], 0.0)
         warm_column = consts.tile([P, 1], F32)
         nc.scalar.activation(out=warm_column[:], in_=zero_column[:], func=ACT.Silu)
+
+        p_codes = consts.tile([P, 2, 64 * 4], U32, align_bytes=64)
+        p_scales = consts.tile([P, 2, 64 * 4], U8, align_bytes=64)
+        v_codes = consts.tile([P, 2, 64], U32, align_bytes=64)
+        v_scales = consts.tile([P, 2, 64], U8, align_bytes=64)
+        nc.vector.memset(p_scales[:].bitcast(I32), 0)
+        nc.vector.memset(v_scales[:].bitcast(I32), 0)
 
         identity = consts.tile([P, P], BF16)
         make_identity(nc, identity[:])
@@ -83,42 +93,36 @@ def tile_pairinteractiongrid_pa_kernel(tc, p, v, W1, b1, W2, b2, out):
                 op=ALU.subtract,
             )
 
-        transposed = psum.tile([P, 2, PACK, P], BF16, tag="layer2")
+        by_k = consts.tile([P, 2, P, PACK], BF16, align_bytes=64)
         for h in range(2):
+            transposed = psum.tile([P, PACK, P], BF16, tag="difference")
             for t in range(PACK):
-                nc.tensor.transpose(transposed[:, h, t, :], inputs_by_row[:, h, t * P : (t + 1) * P], identity[:])
-        b1_transposed = psum.tile([P, P], BF16, tag="difference")
+                nc.tensor.transpose(transposed[:, t, :], inputs_by_row[:, h, t * P : (t + 1) * P], identity[:])
+            copy_out = nc.vector.tensor_copy if h == 0 else nc.scalar.copy
+            copy_out(out=by_k[:, h, :, :], in_=transposed[:].rearrange("q t r -> q r t"))
+        b1_transposed = psum.tile([P, P], BF16, tag="layer2")
         nc.tensor.transpose(b1_transposed[:], b1_rows[:], identity[:])
-        p_by_k = consts.tile([P, P, PACK], BF16, align_bytes=64)
-        v_by_k = consts.tile([P, P, PACK], BF16, align_bytes=64)
-        nc.vector.tensor_copy(
-            out=p_by_k[:].rearrange("q (h r) t -> q h r t", h=2),
-            in_=transposed[:, :, :, 0:64].rearrange("q h t r -> q h r t"),
-        )
-        nc.vector.tensor_copy(
-            out=v_by_k[:].rearrange("q (h r) t -> q h r t", h=2),
-            in_=transposed[:, :, :, 64:128].rearrange("q h t r -> q h r t"),
-        )
         b1_by_group = consts.tile([P, QUARTERS], F32)
         nc.vector.tensor_copy(out=b1_by_group[:], in_=b1_transposed[:, 0:QUARTERS])
 
-        p_fourfold = consts.tile([P, P, 4, PACK], BF16, align_bytes=64)
-        nc.vector.tensor_copy(out=p_fourfold[:], in_=p_by_k[:].unsqueeze(2).to_broadcast([P, P, 4, PACK]))
-        p_codes = consts.tile([P, P * 4], U32, align_bytes=64)
-        p_scales = consts.tile([P, P * 4], U8, align_bytes=64)
-        v_codes = consts.tile([P, P], U32, align_bytes=64)
-        v_scales = consts.tile([P, P], U8, align_bytes=64)
-        nc.vector.memset(p_scales[:].bitcast(I32), 0)
-        nc.vector.memset(v_scales[:].bitcast(I32), 0)
-        nc.vector.quantize_mx(
-            out=v_codes[:].bitcast(FP8X4), scales=v_scales[:], in_=v_by_k[:].rearrange("q r t -> q (r t)")
-        )
-        nc.vector.quantize_mx(
-            out=p_codes[:].bitcast(FP8X4), scales=p_scales[:], in_=p_fourfold[:].rearrange("q r c t -> q (r c t)")
-        )
+        def quantise_inputs(h):
+            p_fourfold = pairs.tile([P, 64, 4, PACK], BF16, align_bytes=64)
+            nc.vector.tensor_copy(
+                out=p_fourfold[:], in_=by_k[:, h, 0:64, :].unsqueeze(2).to_broadcast([P, 64, 4, PACK])
+            )
+            nc.vector.quantize_mx(
+                out=v_codes[:, h, :].bitcast(FP8X4),
+                scales=v_scales[:, h, :],
+                in_=by_k[:, h, 64:128, :].rearrange("q r t -> q (r t)"),
+            )
+            nc.vector.quantize_mx(
+                out=p_codes[:, h, :].bitcast(FP8X4),
+                scales=p_scales[:, h, :],
+                in_=p_fourfold[:].rearrange("q r c t -> q (r c t)"),
+            )
 
-        weight_codes = consts.tile([P, WEIGHT_CHUNKS, F], U32, align_bytes=64)
-        weight_scales = consts.tile([P, WEIGHT_CHUNKS, F], U8, align_bytes=64)
+        weight_codes = consts.tile([P, W2_PIECE + 1, F], U32, align_bytes=64)
+        weight_scales = consts.tile([P, W2_PIECE + 1, F], U8, align_bytes=64)
         weight_grouped = {}
 
         def regroup(copy, grouped, planes):
@@ -128,15 +132,20 @@ def tile_pairinteractiongrid_pa_kernel(tc, p, v, W1, b1, W2, b2, out):
             )
 
         def regroup_weight(w):
-            grouped = weights.tile([P, F, PACK], BF16, align_bytes=64)
-            regroup(nc.vector.tensor_copy if w % 2 == 0 else nc.scalar.copy, grouped[:], weight_raw[w][:])
+            grouped = weights.tile([P, PARTS, P, PACK], BF16, align_bytes=64)
+            for c in range(PARTS):
+                if w == W2_PIECE:
+                    block = weight_raw[PARTS][:, :, c * P : (c + 1) * P]
+                else:
+                    block = weight_raw[c][:, :, w * P : (w + 1) * P]
+                regroup(nc.vector.tensor_copy if c % 2 == 0 else nc.scalar.copy, grouped[:, c, :, :], block)
             weight_grouped[w] = grouped
 
         def quantise_weight(w):
             nc.vector.quantize_mx(
                 out=weight_codes[:, w, :].bitcast(FP8X4),
                 scales=weight_scales[:, w, :],
-                in_=weight_grouped[w][:].rearrange("q f t -> q (f t)"),
+                in_=weight_grouped[w][:].rearrange("q c f t -> q (c f t)"),
             )
 
         p_part = {}
@@ -180,25 +189,27 @@ def tile_pairinteractiongrid_pa_kernel(tc, p, v, W1, b1, W2, b2, out):
             return codes, scales
 
         def multiply(i):
-            step = i // 2
+            h, e = divmod(i // 2, 2)
+            first_p = TILE_POINTS * (i % 4)
+            first_v = 64 + POINTS * e
             values = pairs.tile([P, TILE_POINTS, POINTS, PACK], BF16, align_bytes=64, name="product_values")
             shape = [P, TILE_POINTS, POINTS, PACK]
             nc.vector.tensor_tensor(
                 out=values[:],
-                in0=p_by_k[:, TILE_POINTS * i : TILE_POINTS * (i + 1), :].unsqueeze(2).to_broadcast(shape),
-                in1=v_by_k[:, POINTS * step : POINTS * (step + 1), :].unsqueeze(1).to_broadcast(shape),
+                in0=by_k[:, h, first_p : first_p + TILE_POINTS, :].unsqueeze(2).to_broadcast(shape),
+                in1=by_k[:, h, first_v : first_v + POINTS, :].unsqueeze(1).to_broadcast(shape),
                 op=ALU.mult,
             )
             product_values[i] = values
 
         def spread_p_and_v(i):
-            step, half = divmod(i, 2)
+            h, e = divmod(i // 2, 2)
             codes = pairs.tile([P, TILE_ROWS], U32, align_bytes=64, name="p_part_codes", bufs=3)
             scales = pairs.tile([P, TILE_ROWS], U8, align_bytes=64, name="p_part_scales", bufs=3)
-            first = 4 * TILE_POINTS * i
+            first = 4 * TILE_POINTS * (i % 4)
             nc.vector.tensor_copy(
                 out=codes[:].bitcast(I32).rearrange("q (n r c) -> q n r c", r=8, c=4),
-                in_=p_codes[:, first : first + 4 * TILE_POINTS]
+                in_=p_codes[:, h, first : first + 4 * TILE_POINTS]
                 .bitcast(I32)
                 .rearrange("q (n c) -> q n c", c=4)
                 .unsqueeze(2)
@@ -206,21 +217,21 @@ def tile_pairinteractiongrid_pa_kernel(tc, p, v, W1, b1, W2, b2, out):
             )
             nc.vector.tensor_copy(
                 out=scales[:].bitcast(I32).rearrange("q (n r) -> q n r", r=8),
-                in_=p_scales[:, first : first + 4 * TILE_POINTS].bitcast(I32).unsqueeze(2).to_broadcast([P, TILE_POINTS, 8]),
+                in_=p_scales[:, h, first : first + 4 * TILE_POINTS].bitcast(I32).unsqueeze(2).to_broadcast([P, TILE_POINTS, 8]),
             )
             p_part[i] = (codes, scales)
-            if half == 1:
+            if i % 2 == 1:
                 v_part[i] = v_part[i - 1]
                 return
             codes = pairs.tile([P, TILE_ROWS], U32, align_bytes=64, name="v_part_codes")
             scales = pairs.tile([P, TILE_ROWS], U8, align_bytes=64, name="v_part_scales")
             nc.vector.tensor_copy(
                 out=codes[:].bitcast(I32).rearrange("q (n m) -> q n m", m=POINTS),
-                in_=v_codes[:, POINTS * step : POINTS * (step + 1)].bitcast(I32).unsqueeze(1).to_broadcast([P, TILE_POINTS, POINTS]),
+                in_=v_codes[:, h, POINTS * e : POINTS * (e + 1)].bitcast(I32).unsqueeze(1).to_broadcast([P, TILE_POINTS, POINTS]),
             )
             nc.vector.tensor_copy(
                 out=scales[:].bitcast(I32).rearrange("q (n c) -> q n c", c=POINTS // 4),
-                in_=v_scales[:, POINTS * step : POINTS * (step + 1)].bitcast(I32).unsqueeze(1).to_broadcast([P, TILE_POINTS, POINTS // 4]),
+                in_=v_scales[:, h, POINTS * e : POINTS * (e + 1)].bitcast(I32).unsqueeze(1).to_broadcast([P, TILE_POINTS, POINTS // 4]),
             )
             v_part[i] = (codes, scales)
 
@@ -231,15 +242,15 @@ def tile_pairinteractiongrid_pa_kernel(tc, p, v, W1, b1, W2, b2, out):
                 hidden_planes[i] = planes
             bank = psum.tile([P, TILE_ROWS], F32, tag="layer1", bufs=4)
             parts = [p_part[i], v_part[i], product_part[i], difference_part[i]]
-            for w, (codes, scales) in enumerate(parts):
+            for c, (codes, scales) in enumerate(parts):
                 nc.tensor.matmul_mx(
                     out=bank[:],
-                    lhsT=weight_codes[:, w, j * P : (j + 1) * P].bitcast(FP8X4),
-                    lhsT_scale=weight_scales[:, w, j * P : (j + 1) * P],
+                    lhsT=weight_codes[:, j, c * P : (c + 1) * P].bitcast(FP8X4),
+                    lhsT_scale=weight_scales[:, j, c * P : (c + 1) * P],
                     rhs=codes[:].bitcast(FP8X4),
                     rhs_scale=scales[:],
-                    start=(w == 0),
-                    stop=(w == len(parts) - 1),
+                    start=(c == 0),
+                    stop=(c == PARTS - 1),
                 )
             nc.scalar.activation(
                 out=hidden_planes[i][:, j, :], in_=bank[:], func=ACT.Silu, bias=b1_by_group[:, j : j + 1]
@@ -268,8 +279,8 @@ def tile_pairinteractiongrid_pa_kernel(tc, p, v, W1, b1, W2, b2, out):
                 out=bank[:],
                 lhsT=codes[:, u * P : (u + 1) * P].bitcast(FP8X4),
                 lhsT_scale=scales[:, u * P : (u + 1) * P],
-                rhs=weight_codes[:, W2_CHUNK, :].bitcast(FP8X4),
-                rhs_scale=weight_scales[:, W2_CHUNK, :],
+                rhs=weight_codes[:, W2_PIECE, :].bitcast(FP8X4),
+                rhs_scale=weight_scales[:, W2_PIECE, :],
                 start=True,
                 stop=True,
             )
@@ -285,11 +296,13 @@ def tile_pairinteractiongrid_pa_kernel(tc, p, v, W1, b1, W2, b2, out):
             return i if j == 0 and 0 <= i < TILES else None
 
         for slot in range(-DIFFERENCE_LEAD, UNITS + STORE_LAG):
-            w = slot + DIFFERENCE_LEAD
-            if w < WEIGHT_CHUNKS:
-                regroup_weight(w)
-            if 1 <= w <= WEIGHT_CHUNKS:
-                quantise_weight(w - 1)
+            i = tile_starting_at(slot + INPUT_LEAD)
+            if i is not None and i % 4 == 0:
+                quantise_inputs(i // 4)
+            if 0 <= slot + WEIGHT_LEAD - 1 <= W2_PIECE:
+                quantise_weight(slot + WEIGHT_LEAD - 1)
+            if 0 <= slot + WEIGHT_LEAD <= W2_PIECE:
+                regroup_weight(slot + WEIGHT_LEAD)
 
             if 0 <= slot - STORE_LAG:
                 add_bias_and_store(slot - STORE_LAG)

@@ -27,15 +27,14 @@ UNITS = TILES * QUARTERS
 PARTS = 4
 W2_PIECE = 4
 
-INPUT_LEAD = 7
+INPUT_SLOT = 6
 DIFFERENCE_LEAD = 7
 PRODUCT_LEAD = 6
-WEIGHT_LEAD = 2
 HIDDEN_LAG = 4
-LAYER2_LAG = 6
-STORE_LAG = 7
+LAYER2_LAG = 7
 
-HIDDEN_ROWS_ON_VECTOR = 256
+HALF_ROWS = TILE_ROWS // 2
+LAST = TILES - 1
 
 FLOPS = 2 * STEPS * POINTS * POINTS * (4 * D * F + F * D)
 
@@ -56,13 +55,18 @@ def tile_pairinteractiongrid_pa_kernel(tc, p, v, W1, b1, W2, b2, out):
         stack.enter_context(tc.manual_schedule())
 
         inputs_by_row = consts.tile([P, 2, D], BF16)
-        nc.sync.dma_start(out=inputs_by_row[0:64, :, :], in_=p_rows.rearrange("(h r) d -> r h d", h=2))
-        nc.sync.dma_start(out=inputs_by_row[64:128, :, :], in_=v_rows.rearrange("(h r) d -> r h d", h=2))
+        def load_inputs(h):
+            nc.sync.dma_start(out=inputs_by_row[0:64, h, :], in_=p_rows[64 * h : 64 * (h + 1), :])
+            nc.sync.dma_start(out=inputs_by_row[64:128, h, :], in_=v_rows[64 * h : 64 * (h + 1), :])
+
+        load_inputs(0)
         b1_rows = consts.tile([P, P], BF16)
         nc.gpsimd.memset(b1_rows[:], 0.0)
         nc.sync.dma_start(out=b1_rows[0:PACK, :], in_=b1.rearrange("(t q) -> t q", q=P))
         weight_raw = []
         for c in range(PARTS + 1):
+            if c == PARTS:
+                load_inputs(1)
             rows = W2 if c == PARTS else W1[c * K_PASS : (c + 1) * K_PASS, :]
             raw = weights.tile([P, PACK, F], BF16, bufs=PARTS + 1)
             nc.sync.dma_start(out=raw[:], in_=rows.rearrange("(t q) f -> q t f", q=P))
@@ -85,7 +89,8 @@ def tile_pairinteractiongrid_pa_kernel(tc, p, v, W1, b1, W2, b2, out):
         identity = consts.tile([P, P], BF16)
         make_identity(nc, identity[:])
         chooser = consts.tile([P, 2, POINTS, POINTS], BF16)
-        for e in range(2):
+
+        def make_chooser(e):
             nc.vector.tensor_tensor(
                 out=chooser[:, e, :, :],
                 in0=identity[:, POINTS * e : POINTS * (e + 1)].unsqueeze(2).to_broadcast([P, POINTS, POINTS]),
@@ -94,31 +99,43 @@ def tile_pairinteractiongrid_pa_kernel(tc, p, v, W1, b1, W2, b2, out):
             )
 
         by_k = consts.tile([P, 2, P, PACK], BF16, align_bytes=64)
-        for h in range(2):
-            transposed = psum.tile([P, PACK, P], BF16, tag="difference")
+
+        def transpose_inputs(h, copy_v):
+            transposed = psum.tile([P, PACK, P], BF16, tag="layer1", bufs=4)
             for t in range(PACK):
                 nc.tensor.transpose(transposed[:, t, :], inputs_by_row[:, h, t * P : (t + 1) * P], identity[:])
-            copy_out = nc.vector.tensor_copy if h == 0 else nc.scalar.copy
-            copy_out(out=by_k[:, h, :, :], in_=transposed[:].rearrange("q t r -> q r t"))
-        b1_transposed = psum.tile([P, P], BF16, tag="layer2")
-        nc.tensor.transpose(b1_transposed[:], b1_rows[:], identity[:])
-        b1_by_group = consts.tile([P, QUARTERS], F32)
-        nc.vector.tensor_copy(out=b1_by_group[:], in_=b1_transposed[:, 0:QUARTERS])
+            by_row = transposed[:].rearrange("q t r -> q r t")
+            nc.scalar.copy(out=by_k[:, h, 0:64, :], in_=by_row[:, 0:64, :])
+            copy_v(out=by_k[:, h, 64:128, :], in_=by_row[:, 64:128, :])
 
-        def quantise_inputs(h):
-            p_fourfold = pairs.tile([P, 64, 4, PACK], BF16, align_bytes=64)
+        b1_by_group = consts.tile([P, QUARTERS], F32)
+
+        def transpose_b1():
+            b1_transposed = psum.tile([P, P], BF16, tag="layer2")
+            nc.tensor.transpose(b1_transposed[:], b1_rows[:], identity[:])
+            nc.vector.tensor_copy(out=b1_by_group[:], in_=b1_transposed[:, 0:QUARTERS])
+
+        p_fourfold = {}
+
+        def repeat_p(h):
+            fourfold = pairs.tile([P, 64, 4, PACK], BF16, align_bytes=64)
             nc.vector.tensor_copy(
-                out=p_fourfold[:], in_=by_k[:, h, 0:64, :].unsqueeze(2).to_broadcast([P, 64, 4, PACK])
+                out=fourfold[:], in_=by_k[:, h, 0:64, :].unsqueeze(2).to_broadcast([P, 64, 4, PACK])
             )
+            p_fourfold[h] = fourfold
+
+        def quantise_v(h):
             nc.vector.quantize_mx(
                 out=v_codes[:, h, :].bitcast(FP8X4),
                 scales=v_scales[:, h, :],
                 in_=by_k[:, h, 64:128, :].rearrange("q r t -> q (r t)"),
             )
+
+        def quantise_p(h):
             nc.vector.quantize_mx(
                 out=p_codes[:, h, :].bitcast(FP8X4),
                 scales=p_scales[:, h, :],
-                in_=p_fourfold[:].rearrange("q r c t -> q (r c t)"),
+                in_=p_fourfold[h][:].rearrange("q r c t -> q (r c t)"),
             )
 
         weight_codes = consts.tile([P, W2_PIECE + 1, F], U32, align_bytes=64)
@@ -235,41 +252,51 @@ def tile_pairinteractiongrid_pa_kernel(tc, p, v, W1, b1, W2, b2, out):
             )
             v_part[i] = (codes, scales)
 
-        def layer1_group(unit):
-            i, j = divmod(unit, QUARTERS)
-            if j == 0:
+        def layer1_group(i, j, first, rows):
+            if j == 0 and first == 0:
                 planes = hidden.tile([P, QUARTERS, TILE_ROWS], BF16, name="hidden_planes")
                 hidden_planes[i] = planes
             bank = psum.tile([P, TILE_ROWS], F32, tag="layer1", bufs=4)
             parts = [p_part[i], v_part[i], product_part[i], difference_part[i]]
             for c, (codes, scales) in enumerate(parts):
                 nc.tensor.matmul_mx(
-                    out=bank[:],
+                    out=bank[:, 0:rows],
                     lhsT=weight_codes[:, j, c * P : (c + 1) * P].bitcast(FP8X4),
                     lhsT_scale=weight_scales[:, j, c * P : (c + 1) * P],
-                    rhs=codes[:].bitcast(FP8X4),
-                    rhs_scale=scales[:],
+                    rhs=codes[:, first : first + rows].bitcast(FP8X4),
+                    rhs_scale=scales[:, first : first + rows],
                     start=(c == 0),
                     stop=(c == PARTS - 1),
                 )
             nc.scalar.activation(
-                out=hidden_planes[i][:, j, :], in_=bank[:], func=ACT.Silu, bias=b1_by_group[:, j : j + 1]
+                out=hidden_planes[i][:, j, first : first + rows],
+                in_=bank[:, 0:rows],
+                func=ACT.Silu,
+                bias=b1_by_group[:, j : j + 1],
             )
 
-        def regroup_hidden(i):
-            grouped = hidden.tile([P, TILE_ROWS, PACK], BF16, align_bytes=64, name="hidden_grouped")
-            cut = HIDDEN_ROWS_ON_VECTOR
-            regroup(nc.vector.tensor_copy, grouped[:, 0:cut, :], hidden_planes[i][:, :, 0:cut])
-            regroup(nc.scalar.copy, grouped[:, cut:TILE_ROWS, :], hidden_planes[i][:, :, cut:TILE_ROWS])
-            hidden_grouped[i] = grouped
+        def regroup_hidden(i, copy, first, rows):
+            if i not in hidden_grouped:
+                grouped = hidden.tile([P, TILE_ROWS, PACK], BF16, align_bytes=64, name="hidden_grouped")
+                hidden_grouped[i] = grouped
+            end = first + rows
+            regroup(copy, hidden_grouped[i][:, first:end, :], hidden_planes[i][:, :, first:end])
 
-        def quantise_hidden(i):
-            codes = hidden.tile([P, TILE_ROWS], U32, align_bytes=64, name="hidden_codes")
-            scales = hidden.tile([P, TILE_ROWS], U8, align_bytes=64, name="hidden_scales")
+        def regroup_hidden_shared(i, first, rows):
+            regroup_hidden(i, nc.vector.tensor_copy, first, rows // 2)
+            regroup_hidden(i, nc.scalar.copy, first + rows // 2, rows // 2)
+
+        def quantise_hidden(i, first, rows):
+            if first == 0:
+                codes = hidden.tile([P, TILE_ROWS], U32, align_bytes=64, name="hidden_codes")
+                scales = hidden.tile([P, TILE_ROWS], U8, align_bytes=64, name="hidden_scales")
+                hidden_part[i] = (codes, scales)
+            codes, scales = hidden_part[i]
             nc.vector.quantize_mx(
-                out=codes[:].bitcast(FP8X4), scales=scales[:], in_=hidden_grouped[i][:].rearrange("q r t -> q (r t)")
+                out=codes[:, first : first + rows].bitcast(FP8X4),
+                scales=scales[:, first : first + rows],
+                in_=hidden_grouped[i][:, first : first + rows, :].rearrange("q r t -> q (r t)"),
             )
-            hidden_part[i] = (codes, scales)
 
         def layer2_slice(unit):
             i, u = divmod(unit, QUARTERS)
@@ -295,38 +322,100 @@ def tile_pairinteractiongrid_pa_kernel(tc, p, v, W1, b1, W2, b2, out):
             i, j = divmod(slot, QUARTERS)
             return i if j == 0 and 0 <= i < TILES else None
 
-        for slot in range(-DIFFERENCE_LEAD, UNITS + STORE_LAG):
-            i = tile_starting_at(slot + INPUT_LEAD)
-            if i is not None and i % 4 == 0:
-                quantise_inputs(i // 4)
-            if 0 <= slot + WEIGHT_LEAD - 1 <= W2_PIECE:
-                quantise_weight(slot + WEIGHT_LEAD - 1)
-            if 0 <= slot + WEIGHT_LEAD <= W2_PIECE:
-                regroup_weight(slot + WEIGHT_LEAD)
+        layer2_slices = {}
+        for unit in range(UNITS):
+            i, u = divmod(unit, QUARTERS)
+            layer2_slot = unit + LAYER2_LAG
+            if i == LAST - 1:
+                layer2_slot = UNITS - 3 + (u + 1) // 2
+            elif i == LAST:
+                layer2_slot = UNITS - 1 if u < 2 else UNITS
+            layer2_slices.setdefault(layer2_slot, []).append(unit)
 
-            if 0 <= slot - STORE_LAG:
-                add_bias_and_store(slot - STORE_LAG)
-            if slot + DIFFERENCE_LEAD < UNITS:
-                difference_slice(slot + DIFFERENCE_LEAD)
+        difference_slices = {}
+        for unit in range(QUARTERS, UNITS):
+            slot = max(unit - DIFFERENCE_LEAD, (unit - QUARTERS) // 2)
+            difference_slices.setdefault(slot, []).append(unit)
+        multiply_slots = {max(QUARTERS * i - PRODUCT_LEAD, 0): i for i in range(1, TILES)}
+        product_slots = {max(QUARTERS * i - PRODUCT_LEAD + 1, 1): i for i in range(1, TILES)}
+        difference_slots = {max(QUARTERS * i - PRODUCT_LEAD + 3, 2): i for i in range(1, TILES)}
 
-            i = tile_starting_at(slot + PRODUCT_LEAD)
-            if i is not None:
-                multiply(i)
-            i = tile_starting_at(slot + PRODUCT_LEAD - 1)
-            if i is not None:
-                spread_p_and_v(i)
-                product_part[i] = quantise(product_values[i][:].rearrange("q n m t -> q (n m t)"), "product")
-            i = tile_starting_at(slot + DIFFERENCE_LEAD - QUARTERS)
-            if i is not None:
-                difference_part[i] = quantise(difference_values[i][:].rearrange("q r t -> q (r t)"), "difference")
-            i = tile_starting_at(slot - HIDDEN_LAG)
-            if i is not None:
-                regroup_hidden(i)
-            i = tile_starting_at(slot - HIDDEN_LAG - 1)
-            if i is not None:
-                quantise_hidden(i)
+        def quantise_product(i):
+            product_part[i] = quantise(product_values[i][:].rearrange("q n m t -> q (n m t)"), "product")
+
+        def quantise_difference(i):
+            difference_part[i] = quantise(difference_values[i][:].rearrange("q r t -> q (r t)"), "difference")
+
+        make_chooser(0)
+        transpose_inputs(0, nc.vector.tensor_copy)
+        for unit in range(QUARTERS):
+            difference_slice(unit)
+            if unit == 1:
+                transpose_b1()
+                repeat_p(0)
+                quantise_v(0)
+                multiply(0)
+                quantise_p(0)
+                regroup_weight(0)
+        quantise_product(0)
+        spread_p_and_v(0)
+        quantise_weight(0)
+        quantise_difference(0)
+
+        for slot in range(UNITS + 2):
+            if slot == INPUT_SLOT:
+                transpose_inputs(1, nc.scalar.copy)
+            if slot == INPUT_SLOT + 2:
+                repeat_p(1)
+                quantise_v(1)
+            if slot == INPUT_SLOT + 3:
+                quantise_p(1)
+            if slot < W2_PIECE:
+                regroup_weight(slot + 1)
+
+            stored = layer2_slices.get(slot - 1, [])
+            last_first = {UNITS - 2: 0, UNITS: HALF_ROWS}.get(slot)
+            for unit in stored[:-1]:
+                add_bias_and_store(unit)
+            if last_first is not None:
+                regroup_hidden_shared(LAST, last_first, HALF_ROWS)
+            for unit in stored[-1:]:
+                add_bias_and_store(unit)
+            if last_first is not None:
+                quantise_hidden(LAST, last_first, HALF_ROWS)
+            for unit in difference_slices.get(slot, []):
+                difference_slice(unit)
+
+            if slot in multiply_slots:
+                multiply(multiply_slots[slot])
+            if slot == 0:
+                make_chooser(1)
+            if slot in product_slots:
+                spread_p_and_v(product_slots[slot])
+                quantise_product(product_slots[slot])
+            if slot in difference_slots:
+                quantise_difference(difference_slots[slot])
+            if slot < W2_PIECE:
+                quantise_weight(slot + 1)
+            i, u = divmod(slot - HIDDEN_LAG, QUARTERS)
+            if i == LAST - 1 and u == 0:
+                regroup_hidden_shared(i, 0, TILE_ROWS)
+            elif i == LAST - 1 and u == 1:
+                quantise_hidden(i, 0, TILE_ROWS)
+            elif 0 <= i < LAST - 1:
+                if u == 0:
+                    regroup_hidden(i, nc.vector.tensor_copy, 0, P)
+                if u < QUARTERS - 1:
+                    regroup_hidden(i, nc.scalar.copy, (u + 1) * P, P)
+                else:
+                    quantise_hidden(i, 0, TILE_ROWS)
 
             if 0 <= slot < UNITS:
-                layer1_group(slot)
-            if 0 <= slot - LAYER2_LAG < UNITS:
-                layer2_slice(slot - LAYER2_LAG)
+                i, j = divmod(slot, QUARTERS)
+                if i != LAST:
+                    layer1_group(i, j, 0, TILE_ROWS)
+                else:
+                    for group in (2 * (j % 2), 2 * (j % 2) + 1):
+                        layer1_group(i, group, j // 2 * HALF_ROWS, HALF_ROWS)
+            for unit in layer2_slices.get(slot, []):
+                layer2_slice(unit)

@@ -31,7 +31,7 @@ INPUT_SLOT = 6
 DIFFERENCE_LEAD = 7
 PRODUCT_LEAD = 6
 HIDDEN_LAG = 4
-LAYER2_LAG = 7
+LAYER2_LAG = 8
 
 HALF_ROWS = TILE_ROWS // 2
 LAST = TILES - 1
@@ -55,22 +55,35 @@ def tile_pairinteractiongrid_pa_kernel(tc, p, v, W1, b1, W2, b2, out):
         stack.enter_context(tc.manual_schedule())
 
         inputs_by_row = consts.tile([P, 2, D], BF16)
+        odd_inputs_by_row = consts.tile([P, 2, D], BF16)
+
         def load_inputs(h):
             nc.sync.dma_start(out=inputs_by_row[0:64, h, :], in_=p_rows[64 * h : 64 * (h + 1), :])
             nc.sync.dma_start(out=inputs_by_row[64:128, h, :], in_=v_rows[64 * h : 64 * (h + 1), :])
 
-        load_inputs(0)
+        def load_odd_inputs(h):
+            odd_rows = slice(64 * h + POINTS, 64 * (h + 1))
+            nc.sync.dma_start(out=odd_inputs_by_row[0:POINTS, h, :], in_=p_rows[odd_rows, :])
+            nc.sync.dma_start(out=odd_inputs_by_row[64 : 64 + POINTS, h, :], in_=v_rows[odd_rows, :])
+
         b1_rows = consts.tile([P, P], BF16)
+        identity = consts.tile([P, P], BF16)
+        make_identity(nc, identity[:])
         nc.gpsimd.memset(b1_rows[:], 0.0)
-        nc.sync.dma_start(out=b1_rows[0:PACK, :], in_=b1.rearrange("(t q) -> t q", q=P))
+        nc.gpsimd.memset(odd_inputs_by_row[:].bitcast(F32), 0.0)
+        load_inputs(0)
         weight_raw = []
         for c in range(PARTS + 1):
+            if c == 2:
+                nc.sync.dma_start(out=b1_rows[0:PACK, :], in_=b1.rearrange("(t q) -> t q", q=P))
             if c == PARTS:
+                load_odd_inputs(0)
                 load_inputs(1)
             rows = W2 if c == PARTS else W1[c * K_PASS : (c + 1) * K_PASS, :]
             raw = weights.tile([P, PACK, F], BF16, bufs=PARTS + 1)
             nc.sync.dma_start(out=raw[:], in_=rows.rearrange("(t q) f -> q t f", q=P))
             weight_raw.append(raw)
+        load_odd_inputs(1)
         b2_everywhere = consts.tile([P, D], BF16)
         nc.sync.dma_start(out=b2_everywhere[:], in_=b2.partition_broadcast(P))
 
@@ -86,17 +99,13 @@ def tile_pairinteractiongrid_pa_kernel(tc, p, v, W1, b1, W2, b2, out):
         nc.vector.memset(p_scales[:].bitcast(I32), 0)
         nc.vector.memset(v_scales[:].bitcast(I32), 0)
 
-        identity = consts.tile([P, P], BF16)
-        make_identity(nc, identity[:])
-        chooser = consts.tile([P, 2, POINTS, POINTS], BF16)
-
-        def make_chooser(e):
-            nc.vector.tensor_tensor(
-                out=chooser[:, e, :, :],
-                in0=identity[:, POINTS * e : POINTS * (e + 1)].unsqueeze(2).to_broadcast([P, POINTS, POINTS]),
-                in1=identity[:, 64 + POINTS * e : 64 + POINTS * (e + 1)].unsqueeze(1).to_broadcast([P, POINTS, POINTS]),
-                op=ALU.subtract,
-            )
+        chooser = consts.tile([P, POINTS, POINTS], BF16)
+        nc.vector.tensor_tensor(
+            out=chooser[:],
+            in0=identity[:, 0:POINTS].unsqueeze(2).to_broadcast([P, POINTS, POINTS]),
+            in1=identity[:, 64 : 64 + POINTS].unsqueeze(1).to_broadcast([P, POINTS, POINTS]),
+            op=ALU.subtract,
+        )
 
         by_k = consts.tile([P, 2, P, PACK], BF16, align_bytes=64)
 
@@ -184,12 +193,13 @@ def tile_pairinteractiongrid_pa_kernel(tc, p, v, W1, b1, W2, b2, out):
                 values = pairs.tile([P, TILE_ROWS, PACK], BF16, align_bytes=64, name="difference_values")
                 difference_values[i] = values
             first_point = TILE_POINTS * half + 4 * u
+            rows = (odd_inputs_by_row if e else inputs_by_row)[:, h, :]
             bank = psum.tile([P, PACK, P], F32, tag="difference")
             for t in range(PACK):
                 nc.tensor.matmul(
                     out=bank[:, t, :],
-                    lhsT=inputs_by_row[:, h, t * P : (t + 1) * P],
-                    rhs=chooser[:, e, first_point : first_point + 4, :].rearrange("k n m -> k (n m)"),
+                    lhsT=rows[:, t * P : (t + 1) * P],
+                    rhs=chooser[:, first_point : first_point + 4, :].rearrange("k n m -> k (n m)"),
                     start=True,
                     stop=True,
                 )
@@ -242,11 +252,12 @@ def tile_pairinteractiongrid_pa_kernel(tc, p, v, W1, b1, W2, b2, out):
                 return
             codes = pairs.tile([P, TILE_ROWS], U32, align_bytes=64, name="v_part_codes")
             scales = pairs.tile([P, TILE_ROWS], U8, align_bytes=64, name="v_part_scales")
-            nc.vector.tensor_copy(
+            move = nc.vector.tensor_copy if i == 0 else nc.sync.dma_start
+            move(
                 out=codes[:].bitcast(I32).rearrange("q (n m) -> q n m", m=POINTS),
                 in_=v_codes[:, h, POINTS * e : POINTS * (e + 1)].bitcast(I32).unsqueeze(1).to_broadcast([P, TILE_POINTS, POINTS]),
             )
-            nc.vector.tensor_copy(
+            move(
                 out=scales[:].bitcast(I32).rearrange("q (n c) -> q n c", c=POINTS // 4),
                 in_=v_scales[:, h, POINTS * e : POINTS * (e + 1)].bitcast(I32).unsqueeze(1).to_broadcast([P, TILE_POINTS, POINTS // 4]),
             )
@@ -326,7 +337,9 @@ def tile_pairinteractiongrid_pa_kernel(tc, p, v, W1, b1, W2, b2, out):
         for unit in range(UNITS):
             i, u = divmod(unit, QUARTERS)
             layer2_slot = unit + LAYER2_LAG
-            if i == LAST - 1:
+            if i == LAST - 2:
+                layer2_slot = unit + 6
+            elif i == LAST - 1:
                 layer2_slot = UNITS - 3 + (u + 1) // 2
             elif i == LAST:
                 layer2_slot = UNITS - 1 if u < 2 else UNITS
@@ -346,12 +359,10 @@ def tile_pairinteractiongrid_pa_kernel(tc, p, v, W1, b1, W2, b2, out):
         def quantise_difference(i):
             difference_part[i] = quantise(difference_values[i][:].rearrange("q r t -> q (r t)"), "difference")
 
-        make_chooser(0)
         transpose_inputs(0, nc.vector.tensor_copy)
         for unit in range(QUARTERS):
             difference_slice(unit)
             if unit == 1:
-                transpose_b1()
                 repeat_p(0)
                 quantise_v(0)
                 multiply(0)
@@ -359,6 +370,7 @@ def tile_pairinteractiongrid_pa_kernel(tc, p, v, W1, b1, W2, b2, out):
                 regroup_weight(0)
         quantise_product(0)
         spread_p_and_v(0)
+        transpose_b1()
         quantise_weight(0)
         quantise_difference(0)
 
@@ -388,8 +400,6 @@ def tile_pairinteractiongrid_pa_kernel(tc, p, v, W1, b1, W2, b2, out):
 
             if slot in multiply_slots:
                 multiply(multiply_slots[slot])
-            if slot == 0:
-                make_chooser(1)
             if slot in product_slots:
                 spread_p_and_v(product_slots[slot])
                 quantise_product(product_slots[slot])
@@ -398,11 +408,12 @@ def tile_pairinteractiongrid_pa_kernel(tc, p, v, W1, b1, W2, b2, out):
             if slot < W2_PIECE:
                 quantise_weight(slot + 1)
             i, u = divmod(slot - HIDDEN_LAG, QUARTERS)
-            if i == LAST - 1 and u == 0:
-                regroup_hidden_shared(i, 0, TILE_ROWS)
-            elif i == LAST - 1 and u == 1:
-                quantise_hidden(i, 0, TILE_ROWS)
-            elif 0 <= i < LAST - 1:
+            if LAST - 2 <= i < LAST:
+                if u == 0:
+                    regroup_hidden_shared(i, 0, TILE_ROWS)
+                elif u == 1:
+                    quantise_hidden(i, 0, TILE_ROWS)
+            elif 0 <= i < LAST - 2:
                 if u == 0:
                     regroup_hidden(i, nc.vector.tensor_copy, 0, P)
                 if u < QUARTERS - 1:

@@ -92,10 +92,10 @@ def tile_pairinteractiongrid_pa_kernel(tc, p, v, W1, b1, W2, b2, out):
         warm_column = consts.tile([P, 1], F32)
         nc.scalar.activation(out=warm_column[:], in_=zero_column[:], func=ACT.Silu)
 
-        p_codes = consts.tile([P, 2, 64 * 4], U32, align_bytes=64)
-        p_scales = consts.tile([P, 2, 64 * 4], U8, align_bytes=64)
-        v_codes = consts.tile([P, 2, 64], U32, align_bytes=64)
-        v_scales = consts.tile([P, 2, 64], U8, align_bytes=64)
+        p_codes = consts.tile([P, 2, 64 * 4], U32, align_bytes=256)
+        p_scales = consts.tile([P, 2, 64 * 4], U8, align_bytes=256)
+        v_codes = consts.tile([P, 2, 64], U32, align_bytes=256)
+        v_scales = consts.tile([P, 2, 64], U8, align_bytes=256)
         nc.vector.memset(p_scales[:].bitcast(I32), 0)
         nc.vector.memset(v_scales[:].bitcast(I32), 0)
 
@@ -147,8 +147,8 @@ def tile_pairinteractiongrid_pa_kernel(tc, p, v, W1, b1, W2, b2, out):
                 in_=p_fourfold[h][:].rearrange("q r c t -> q (r c t)"),
             )
 
-        weight_codes = consts.tile([P, W2_PIECE + 1, F], U32, align_bytes=64)
-        weight_scales = consts.tile([P, W2_PIECE + 1, F], U8, align_bytes=64)
+        weight_codes = consts.tile([P, W2_PIECE + 1, F], U32, align_bytes=256)
+        weight_scales = consts.tile([P, W2_PIECE + 1, F], U8, align_bytes=256)
         weight_grouped = {}
 
         def regroup(copy, grouped, planes):
@@ -210,8 +210,8 @@ def tile_pairinteractiongrid_pa_kernel(tc, p, v, W1, b1, W2, b2, out):
             )
 
         def quantise(values, name):
-            codes = pairs.tile([P, TILE_ROWS], U32, align_bytes=64, name=name + "_codes", bufs=3)
-            scales = pairs.tile([P, TILE_ROWS], U8, align_bytes=64, name=name + "_scales", bufs=3)
+            codes = pairs.tile([P, TILE_ROWS], U32, align_bytes=256, name=name + "_codes", bufs=3)
+            scales = pairs.tile([P, TILE_ROWS], U8, align_bytes=256, name=name + "_scales", bufs=3)
             nc.vector.quantize_mx(out=codes[:].bitcast(FP8X4), scales=scales[:], in_=values)
             return codes, scales
 
@@ -231,8 +231,8 @@ def tile_pairinteractiongrid_pa_kernel(tc, p, v, W1, b1, W2, b2, out):
 
         def spread_p_and_v(i):
             h, e = divmod(i // 2, 2)
-            codes = pairs.tile([P, TILE_ROWS], U32, align_bytes=64, name="p_part_codes", bufs=3)
-            scales = pairs.tile([P, TILE_ROWS], U8, align_bytes=64, name="p_part_scales", bufs=3)
+            codes = pairs.tile([P, TILE_ROWS], U32, align_bytes=256, name="p_part_codes", bufs=3)
+            scales = pairs.tile([P, TILE_ROWS], U8, align_bytes=256, name="p_part_scales", bufs=3)
             first = 4 * TILE_POINTS * (i % 4)
             nc.vector.tensor_copy(
                 out=codes[:].bitcast(I32).rearrange("q (n r c) -> q n r c", r=8, c=4),
@@ -250,8 +250,8 @@ def tile_pairinteractiongrid_pa_kernel(tc, p, v, W1, b1, W2, b2, out):
             if i % 2 == 1:
                 v_part[i] = v_part[i - 1]
                 return
-            codes = pairs.tile([P, TILE_ROWS], U32, align_bytes=64, name="v_part_codes")
-            scales = pairs.tile([P, TILE_ROWS], U8, align_bytes=64, name="v_part_scales")
+            codes = pairs.tile([P, TILE_ROWS], U32, align_bytes=256, name="v_part_codes")
+            scales = pairs.tile([P, TILE_ROWS], U8, align_bytes=256, name="v_part_scales")
             move = nc.vector.tensor_copy if i == 0 else nc.sync.dma_start
             move(
                 out=codes[:].bitcast(I32).rearrange("q (n m) -> q n m", m=POINTS),
@@ -299,8 +299,8 @@ def tile_pairinteractiongrid_pa_kernel(tc, p, v, W1, b1, W2, b2, out):
 
         def quantise_hidden(i, first, rows):
             if first == 0:
-                codes = hidden.tile([P, TILE_ROWS], U32, align_bytes=64, name="hidden_codes")
-                scales = hidden.tile([P, TILE_ROWS], U8, align_bytes=64, name="hidden_scales")
+                codes = hidden.tile([P, TILE_ROWS], U32, align_bytes=256, name="hidden_codes")
+                scales = hidden.tile([P, TILE_ROWS], U8, align_bytes=256, name="hidden_scales")
                 hidden_part[i] = (codes, scales)
             codes, scales = hidden_part[i]
             nc.vector.quantize_mx(

@@ -35,6 +35,11 @@ LAYER2_LAG = 8
 
 HALF_ROWS = TILE_ROWS // 2
 LAST = TILES - 1
+VD = (0, 0, 0, 2, 2, 2, 2, 2)
+WSC = ((1, 3), (1, 3), (1, 3), (1, 3), (1,))
+HV = (4, 2, 1, 1, 1, 1, 1, 1)
+DQ = 3
+EARLY_PIECES = 2
 
 FLOPS = 2 * STEPS * POINTS * POINTS * (4 * D * F + F * D)
 
@@ -157,15 +162,16 @@ def tile_pairinteractiongrid_pa_kernel(tc, p, v, W1, b1, W2, b2, out):
                 in_=planes.rearrange("q t (c i) -> q c t i", i=4),
             )
 
-        def regroup_weight(w):
-            grouped = weights.tile([P, PARTS, P, PACK], BF16, align_bytes=64)
-            for c in range(PARTS):
+        def regroup_weight(w, cs=(0, 1, 2, 3)):
+            if w not in weight_grouped:
+                grouped = weights.tile([P, PARTS, P, PACK], BF16, align_bytes=64)
+                weight_grouped[w] = grouped
+            for c in cs:
                 if w == W2_PIECE:
                     block = weight_raw[PARTS][:, :, c * P : (c + 1) * P]
                 else:
                     block = weight_raw[c][:, :, w * P : (w + 1) * P]
-                regroup(nc.vector.tensor_copy if c % 2 == 0 else nc.scalar.copy, grouped[:, c, :, :], block)
-            weight_grouped[w] = grouped
+                regroup(nc.scalar.copy if c in WSC[w] else nc.vector.tensor_copy, weight_grouped[w][:, c, :, :], block)
 
         def quantise_weight(w):
             nc.vector.quantize_mx(
@@ -192,6 +198,25 @@ def tile_pairinteractiongrid_pa_kernel(tc, p, v, W1, b1, W2, b2, out):
             if u == 0:
                 values = pairs.tile([P, TILE_ROWS, PACK], BF16, align_bytes=64, name="difference_values")
                 difference_values[i] = values
+            if u < VD[i]:
+                if u == 0:
+                    points = 4 * VD[i]
+                    first_p = POINTS * e + TILE_POINTS * half
+                    first_v = 64 + POINTS * e
+                    shape = [P, points, POINTS, PACK]
+                    signed = pairs.tile([P, TILE_POINTS, POINTS, PACK], BF16, align_bytes=64)
+                    nc.vector.tensor_tensor(
+                        out=signed[:, 0:points, :, :],
+                        in0=by_k[:, h, first_p : first_p + points, :].unsqueeze(2).to_broadcast(shape),
+                        in1=by_k[:, h, first_v : first_v + POINTS, :].unsqueeze(1).to_broadcast(shape),
+                        op=ALU.subtract,
+                    )
+                    nc.scalar.activation(
+                        out=difference_values[i][:, 0 : VD[i] * P, :],
+                        in_=signed[:, 0:points, :, :].rearrange("q n m t -> q (n m) t"),
+                        func=ACT.Abs,
+                    )
+                return
             first_point = TILE_POINTS * half + 4 * u
             rows = (odd_inputs_by_row if e else inputs_by_row)[:, h, :]
             bank = psum.tile([P, PACK, P], F32, tag="difference")
@@ -351,7 +376,7 @@ def tile_pairinteractiongrid_pa_kernel(tc, p, v, W1, b1, W2, b2, out):
             difference_slices.setdefault(slot, []).append(unit)
         multiply_slots = {max(QUARTERS * i - PRODUCT_LEAD, 0): i for i in range(1, TILES)}
         product_slots = {max(QUARTERS * i - PRODUCT_LEAD + 1, 1): i for i in range(1, TILES)}
-        difference_slots = {max(QUARTERS * i - PRODUCT_LEAD + 3, 2): i for i in range(1, TILES)}
+        difference_slots = {max(QUARTERS * i - DQ, 2): i for i in range(1, TILES)}
 
         def quantise_product(i):
             product_part[i] = quantise(product_values[i][:].rearrange("q n m t -> q (n m t)"), "product")
@@ -359,15 +384,19 @@ def tile_pairinteractiongrid_pa_kernel(tc, p, v, W1, b1, W2, b2, out):
         def quantise_difference(i):
             difference_part[i] = quantise(difference_values[i][:].rearrange("q r t -> q (r t)"), "difference")
 
+        for w in range(EARLY_PIECES):
+            regroup_weight(w, (0,))
         transpose_inputs(0, nc.vector.tensor_copy)
-        for unit in range(QUARTERS):
-            difference_slice(unit)
-            if unit == 1:
-                repeat_p(0)
-                quantise_v(0)
-                multiply(0)
-                quantise_p(0)
-                regroup_weight(0)
+        repeat_p(0)
+        quantise_v(0)
+        multiply(0)
+        quantise_p(0)
+        difference_slice(0)
+        difference_slice(1)
+        regroup_weight(0, (1, 2))
+        difference_slice(2)
+        difference_slice(3)
+        regroup_weight(0, (3,))
         quantise_product(0)
         spread_p_and_v(0)
         transpose_b1()
@@ -383,8 +412,12 @@ def tile_pairinteractiongrid_pa_kernel(tc, p, v, W1, b1, W2, b2, out):
             if slot == INPUT_SLOT + 3:
                 quantise_p(1)
             if slot < W2_PIECE:
-                regroup_weight(slot + 1)
+                regroup_weight(slot + 1, (1, 2, 3) if slot + 1 < EARLY_PIECES else (0, 1, 2, 3))
 
+            for unit in difference_slices.get(slot, []):
+                difference_slice(unit)
+            if slot in multiply_slots:
+                multiply(multiply_slots[slot])
             stored = layer2_slices.get(slot - 1, [])
             last_first = {UNITS - 2: 0, UNITS: HALF_ROWS}.get(slot)
             for unit in stored[:-1]:
@@ -395,11 +428,6 @@ def tile_pairinteractiongrid_pa_kernel(tc, p, v, W1, b1, W2, b2, out):
                 add_bias_and_store(unit)
             if last_first is not None:
                 quantise_hidden(LAST, last_first, HALF_ROWS)
-            for unit in difference_slices.get(slot, []):
-                difference_slice(unit)
-
-            if slot in multiply_slots:
-                multiply(multiply_slots[slot])
             if slot in product_slots:
                 spread_p_and_v(product_slots[slot])
                 quantise_product(product_slots[slot])
@@ -415,10 +443,10 @@ def tile_pairinteractiongrid_pa_kernel(tc, p, v, W1, b1, W2, b2, out):
                     quantise_hidden(i, 0, TILE_ROWS)
             elif 0 <= i < LAST - 2:
                 if u == 0:
-                    regroup_hidden(i, nc.vector.tensor_copy, 0, P)
-                if u < QUARTERS - 1:
-                    regroup_hidden(i, nc.scalar.copy, (u + 1) * P, P)
-                else:
+                    regroup_hidden(i, nc.vector.tensor_copy, 0, P * HV[i])
+                if u < QUARTERS - HV[i]:
+                    regroup_hidden(i, nc.scalar.copy, (u + HV[i]) * P, P)
+                if u == 3:
                     quantise_hidden(i, 0, TILE_ROWS)
 
             if 0 <= slot < UNITS:

@@ -37,9 +37,14 @@ HALF_ROWS = TILE_ROWS // 2
 LAST = TILES - 1
 VD = (0, 0, 0, 2, 2, 2, 2, 2)
 WSC = ((1, 3), (1, 3), (1, 3), (1, 3), (1,))
-HV = (4, 2, 1, 1, 1, 1, 1, 1)
-DQ = 3
+HV = (4, 1, 1, 1, 1, 1, 1, 1)
+DQ = 2
 EARLY_PIECES = 2
+BLOCKS = ((0, 256), (256, 128), (384, 128))
+WORK = {28: [(0, 0), (0, 1)], 29: [(0, 2), (0, 3)], 30: [(1, 0), (1, 1), (1, 2), (1, 3)], 31: [(2, 0), (2, 1), (2, 2), (2, 3)]}
+REG = {30: 0, 31: 1, 32: 2}
+LL = (31, 31, 32, 32)
+AH = {2: (1, 0)}
 
 FLOPS = 2 * STEPS * POINTS * POINTS * (4 * D * F + F * D)
 
@@ -187,6 +192,8 @@ def tile_pairinteractiongrid_pa_kernel(tc, p, v, W1, b1, W2, b2, out):
         product_values = {}
         difference_values = {}
         hidden_planes = {}
+        signed_values = {}
+        layer1_banks = {}
         hidden_grouped = {}
         hidden_part = {}
         layer2_banks = {}
@@ -211,9 +218,11 @@ def tile_pairinteractiongrid_pa_kernel(tc, p, v, W1, b1, W2, b2, out):
                         in1=by_k[:, h, first_v : first_v + POINTS, :].unsqueeze(1).to_broadcast(shape),
                         op=ALU.subtract,
                     )
+                    signed_values[i] = signed
+                if u == VD[i] - 1:
                     nc.scalar.activation(
                         out=difference_values[i][:, 0 : VD[i] * P, :],
-                        in_=signed[:, 0:points, :, :].rearrange("q n m t -> q (n m) t"),
+                        in_=signed_values[i][:, 0 : 4 * VD[i], :, :].rearrange("q n m t -> q (n m) t"),
                         func=ACT.Abs,
                     )
                 return
@@ -288,13 +297,13 @@ def tile_pairinteractiongrid_pa_kernel(tc, p, v, W1, b1, W2, b2, out):
             )
             v_part[i] = (codes, scales)
 
-        def layer1_group(i, j, first, rows):
-            if j == 0 and first == 0:
-                planes = hidden.tile([P, QUARTERS, TILE_ROWS], BF16, name="hidden_planes")
-                hidden_planes[i] = planes
-            bank = psum.tile([P, TILE_ROWS], F32, tag="layer1", bufs=4)
-            parts = [p_part[i], v_part[i], product_part[i], difference_part[i]]
-            for c, (codes, scales) in enumerate(parts):
+        def layer1_passes(i, j, first, rows, cs):
+            if cs[0] == 0:
+                bank = psum.tile([P, TILE_ROWS], F32, tag="layer1", bufs=4)
+                layer1_banks[i, j] = bank
+            bank = layer1_banks[i, j]
+            for c in cs:
+                codes, scales = [p_part, v_part, product_part, difference_part][c][i]
                 nc.tensor.matmul_mx(
                     out=bank[:, 0:rows],
                     lhsT=weight_codes[:, j, c * P : (c + 1) * P].bitcast(FP8X4),
@@ -304,6 +313,15 @@ def tile_pairinteractiongrid_pa_kernel(tc, p, v, W1, b1, W2, b2, out):
                     start=(c == 0),
                     stop=(c == PARTS - 1),
                 )
+
+        def layer1_group(i, j, first, rows):
+            if j == 0 and first == 0:
+                planes = hidden.tile([P, QUARTERS, TILE_ROWS], BF16, name="hidden_planes")
+                hidden_planes[i] = planes
+            if (i, j) not in layer1_banks:
+                layer1_passes(i, j, first, rows, (0, 1))
+            layer1_passes(i, j, first, rows, (2, 3))
+            bank = layer1_banks.pop((i, j))
             nc.scalar.activation(
                 out=hidden_planes[i][:, j, first : first + rows],
                 in_=bank[:, 0:rows],
@@ -367,7 +385,7 @@ def tile_pairinteractiongrid_pa_kernel(tc, p, v, W1, b1, W2, b2, out):
             elif i == LAST - 1:
                 layer2_slot = UNITS - 3 + (u + 1) // 2
             elif i == LAST:
-                layer2_slot = UNITS - 1 if u < 2 else UNITS
+                layer2_slot = LL[u]
             layer2_slices.setdefault(layer2_slot, []).append(unit)
 
         difference_slices = {}
@@ -419,15 +437,15 @@ def tile_pairinteractiongrid_pa_kernel(tc, p, v, W1, b1, W2, b2, out):
             if slot in multiply_slots:
                 multiply(multiply_slots[slot])
             stored = layer2_slices.get(slot - 1, [])
-            last_first = {UNITS - 2: 0, UNITS: HALF_ROWS}.get(slot)
+            last_block = BLOCKS[REG[slot]] if slot in REG else None
             for unit in stored[:-1]:
                 add_bias_and_store(unit)
-            if last_first is not None:
-                regroup_hidden_shared(LAST, last_first, HALF_ROWS)
+            if last_block is not None:
+                regroup_hidden_shared(LAST, *last_block)
             for unit in stored[-1:]:
                 add_bias_and_store(unit)
-            if last_first is not None:
-                quantise_hidden(LAST, last_first, HALF_ROWS)
+            if last_block is not None:
+                quantise_hidden(LAST, *last_block)
             if slot in product_slots:
                 spread_p_and_v(product_slots[slot])
                 quantise_product(product_slots[slot])
@@ -442,19 +460,22 @@ def tile_pairinteractiongrid_pa_kernel(tc, p, v, W1, b1, W2, b2, out):
                 elif u == 1:
                     quantise_hidden(i, 0, TILE_ROWS)
             elif 0 <= i < LAST - 2:
-                if u == 0:
+                if u == 0 and HV[i] > 0:
                     regroup_hidden(i, nc.vector.tensor_copy, 0, P * HV[i])
-                if u < QUARTERS - HV[i]:
-                    regroup_hidden(i, nc.scalar.copy, (u + HV[i]) * P, P)
+                for s in range(HV[i], QUARTERS):
+                    if max(s - 1, 0) == u:
+                        regroup_hidden(i, nc.scalar.copy, s * P, P)
                 if u == 3:
                     quantise_hidden(i, 0, TILE_ROWS)
 
             if 0 <= slot < UNITS:
                 i, j = divmod(slot, QUARTERS)
+                if slot in AH:
+                    layer1_passes(*AH[slot], 0, TILE_ROWS, (0, 1))
                 if i != LAST:
                     layer1_group(i, j, 0, TILE_ROWS)
                 else:
-                    for group in (2 * (j % 2), 2 * (j % 2) + 1):
-                        layer1_group(i, group, j // 2 * HALF_ROWS, HALF_ROWS)
+                    for b, group in WORK[slot]:
+                        layer1_group(i, group, *BLOCKS[b])
             for unit in layer2_slices.get(slot, []):
                 layer2_slice(unit)

@@ -44,6 +44,8 @@ BLOCKS = ((0, 256), (256, 128), (384, 128))
 WORK = {28: [(0, 0), (0, 1)], 29: [(0, 2), (0, 3)], 30: [(1, 0), (1, 1), (1, 2), (1, 3)], 31: [(2, 0), (2, 1), (2, 2), (2, 3)]}
 REG = {30: 0, 31: 1, 32: 2}
 LL = (31, 31, 32, 32)
+PBS = 16
+HB = (6, 7)
 AH = {2: (1, 0)}
 
 FLOPS = 2 * STEPS * POINTS * POINTS * (4 * D * F + F * D)
@@ -265,6 +267,9 @@ def tile_pairinteractiongrid_pa_kernel(tc, p, v, W1, b1, W2, b2, out):
 
         def spread_p_and_v(i):
             h, e = divmod(i // 2, 2)
+            if i in HB:
+                spread_v(i, h, e)
+                return
             codes = pairs.tile([P, TILE_ROWS], U32, align_bytes=256, name="p_part_codes", bufs=3)
             scales = pairs.tile([P, TILE_ROWS], U8, align_bytes=256, name="p_part_scales", bufs=3)
             first = 4 * TILE_POINTS * (i % 4)
@@ -281,6 +286,9 @@ def tile_pairinteractiongrid_pa_kernel(tc, p, v, W1, b1, W2, b2, out):
                 in_=p_scales[:, h, first : first + 4 * TILE_POINTS].bitcast(I32).unsqueeze(2).to_broadcast([P, TILE_POINTS, 8]),
             )
             p_part[i] = (codes, scales)
+            spread_v(i, h, e)
+
+        def spread_v(i, h, e):
             if i % 2 == 1:
                 v_part[i] = v_part[i - 1]
                 return
@@ -297,12 +305,36 @@ def tile_pairinteractiongrid_pa_kernel(tc, p, v, W1, b1, W2, b2, out):
             )
             v_part[i] = (codes, scales)
 
+        p_bias = consts.tile([P, QUARTERS, POINTS], F32)
+
+        def make_p_bias():
+            bank = psum.tile([P, QUARTERS, P], F32, tag="difference")
+            for j in range(QUARTERS):
+                nc.tensor.matmul_mx(
+                    out=bank[:, j, :],
+                    lhsT=weight_codes[:, j, 0:P].bitcast(FP8X4),
+                    lhsT_scale=weight_scales[:, j, 0:P],
+                    rhs=p_codes[:, 1, P : 2 * P].bitcast(FP8X4),
+                    rhs_scale=p_scales[:, 1, P : 2 * P],
+                    start=True,
+                    stop=True,
+                )
+            for j in range(QUARTERS):
+                nc.scalar.activation(
+                    out=p_bias[:, j, :],
+                    in_=bank[:, j, :].rearrange("q (n c) -> q n c", c=4)[:, :, 0],
+                    func=ACT.Identity,
+                    bias=b1_by_group[:, j : j + 1],
+                )
+
         def layer1_passes(i, j, first, rows, cs):
-            if cs[0] == 0:
+            if (i, j, first) not in layer1_banks:
                 bank = psum.tile([P, TILE_ROWS], F32, tag="layer1", bufs=4)
-                layer1_banks[i, j] = bank
-            bank = layer1_banks[i, j]
+                layer1_banks[i, j, first] = bank
+            bank = layer1_banks[i, j, first]
             for c in cs:
+                if c == 0 and i in HB:
+                    continue
                 codes, scales = [p_part, v_part, product_part, difference_part][c][i]
                 nc.tensor.matmul_mx(
                     out=bank[:, 0:rows],
@@ -310,7 +342,7 @@ def tile_pairinteractiongrid_pa_kernel(tc, p, v, W1, b1, W2, b2, out):
                     lhsT_scale=weight_scales[:, j, c * P : (c + 1) * P],
                     rhs=codes[:, first : first + rows].bitcast(FP8X4),
                     rhs_scale=scales[:, first : first + rows],
-                    start=(c == 0),
+                    start=(c == (1 if i in HB else 0)),
                     stop=(c == PARTS - 1),
                 )
 
@@ -318,16 +350,26 @@ def tile_pairinteractiongrid_pa_kernel(tc, p, v, W1, b1, W2, b2, out):
             if j == 0 and first == 0:
                 planes = hidden.tile([P, QUARTERS, TILE_ROWS], BF16, name="hidden_planes")
                 hidden_planes[i] = planes
-            if (i, j) not in layer1_banks:
+            if (i, j, first) not in layer1_banks:
                 layer1_passes(i, j, first, rows, (0, 1))
             layer1_passes(i, j, first, rows, (2, 3))
-            bank = layer1_banks.pop((i, j))
-            nc.scalar.activation(
-                out=hidden_planes[i][:, j, first : first + rows],
-                in_=bank[:, 0:rows],
-                func=ACT.Silu,
-                bias=b1_by_group[:, j : j + 1],
-            )
+            bank = layer1_banks[i, j, first]
+            if i in HB:
+                point = TILE_POINTS * (i % 2) + first // POINTS
+                for n in range(rows // POINTS):
+                    nc.scalar.activation(
+                        out=hidden_planes[i][:, j, first + n * POINTS : first + (n + 1) * POINTS],
+                        in_=bank[:, n * POINTS : (n + 1) * POINTS],
+                        func=ACT.Silu,
+                        bias=p_bias[:, j, point + n : point + n + 1],
+                    )
+            else:
+                nc.scalar.activation(
+                    out=hidden_planes[i][:, j, first : first + rows],
+                    in_=bank[:, 0:rows],
+                    func=ACT.Silu,
+                    bias=b1_by_group[:, j : j + 1],
+                )
 
         def regroup_hidden(i, copy, first, rows):
             if i not in hidden_grouped:
@@ -479,3 +521,5 @@ def tile_pairinteractiongrid_pa_kernel(tc, p, v, W1, b1, W2, b2, out):
                         layer1_group(i, group, *BLOCKS[b])
             for unit in layer2_slices.get(slot, []):
                 layer2_slice(unit)
+            if slot == PBS:
+                make_p_bias()

@@ -39,12 +39,19 @@ VD = (0, 0, 0, 2, 2, 2, 2, 2)
 WSC = ((1, 3), (1, 3), (1, 3), (1, 3), (1,))
 HV = (4, 1, 1, 1, 1, 1, 1, 1)
 DQ = 2
-EARLY_PIECES = 2
+EARLY_PIECES = 1
 BLOCKS = ((0, 256), (256, 128), (384, 128))
 WORK = {28: [(0, 0), (0, 1)], 29: [(0, 2), (0, 3)], 30: [(1, 0), (1, 1), (1, 2), (1, 3)], 31: [(2, 0), (2, 1), (2, 2), (2, 3)]}
 REG = {30: 0, 31: 1, 32: 2}
 LL = (31, 31, 32, 32)
-PBS = 16
+SH = (384, 384)
+TD = 28
+RU = (0, 0)
+QU = (1, 1)
+L5 = (26, 27, 28, 29)
+L6 = (29, 30, 30, 31)
+SPL = 2
+PBS = 22
 HB = (6, 7)
 AH = {2: (1, 0)}
 
@@ -305,23 +312,23 @@ def tile_pairinteractiongrid_pa_kernel(tc, p, v, W1, b1, W2, b2, out):
             )
             v_part[i] = (codes, scales)
 
-        p_bias = consts.tile([P, QUARTERS, POINTS], F32)
+        p_bias = consts.tile([P, QUARTERS, 2 * POINTS], F32)
 
-        def make_p_bias():
+        def make_p_bias(e):
             bank = psum.tile([P, QUARTERS, P], F32, tag="difference")
             for j in range(QUARTERS):
                 nc.tensor.matmul_mx(
                     out=bank[:, j, :],
                     lhsT=weight_codes[:, j, 0:P].bitcast(FP8X4),
                     lhsT_scale=weight_scales[:, j, 0:P],
-                    rhs=p_codes[:, 1, P : 2 * P].bitcast(FP8X4),
-                    rhs_scale=p_scales[:, 1, P : 2 * P],
+                    rhs=p_codes[:, 1, P * e : P * (e + 1)].bitcast(FP8X4),
+                    rhs_scale=p_scales[:, 1, P * e : P * (e + 1)],
                     start=True,
                     stop=True,
                 )
             for j in range(QUARTERS):
                 nc.scalar.activation(
-                    out=p_bias[:, j, :],
+                    out=p_bias[:, j, POINTS * e : POINTS * (e + 1)],
                     in_=bank[:, j, :].rearrange("q (n c) -> q n c", c=4)[:, :, 0],
                     func=ACT.Identity,
                     bias=b1_by_group[:, j : j + 1],
@@ -355,7 +362,7 @@ def tile_pairinteractiongrid_pa_kernel(tc, p, v, W1, b1, W2, b2, out):
             layer1_passes(i, j, first, rows, (2, 3))
             bank = layer1_banks[i, j, first]
             if i in HB:
-                point = TILE_POINTS * (i % 2) + first // POINTS
+                point = TILE_POINTS * (i % 4) + first // POINTS
                 for n in range(rows // POINTS):
                     nc.scalar.activation(
                         out=hidden_planes[i][:, j, first + n * POINTS : first + (n + 1) * POINTS],
@@ -397,7 +404,7 @@ def tile_pairinteractiongrid_pa_kernel(tc, p, v, W1, b1, W2, b2, out):
         def layer2_slice(unit):
             i, u = divmod(unit, QUARTERS)
             codes, scales = hidden_part[i]
-            bank = psum.tile([P, D], F32, tag="layer2")
+            bank = psum.tile([P, D], F32, tag="difference" if unit >= TD and unit % 2 else "layer2", name="bank")
             nc.tensor.matmul_mx(
                 out=bank[:],
                 lhsT=codes[:, u * P : (u + 1) * P].bitcast(FP8X4),
@@ -411,8 +418,13 @@ def tile_pairinteractiongrid_pa_kernel(tc, p, v, W1, b1, W2, b2, out):
 
         def add_bias_and_store(unit):
             result = results.tile([P, D], F32)
-            nc.vector.tensor_tensor(out=result[:], in0=layer2_banks[unit][:], in1=b2_everywhere[:], op=ALU.add)
-            nc.sync.dma_start(out=out_rows[unit * P : (unit + 1) * P, :], in_=result[:])
+            width = D // (SPL if unit == UNITS - 1 else 1)
+            for a in range(0, D, width):
+                cols = slice(a, a + width)
+                nc.vector.tensor_tensor(
+                    out=result[:, cols], in0=layer2_banks[unit][:, cols], in1=b2_everywhere[:, cols], op=ALU.add
+                )
+                nc.sync.dma_start(out=out_rows[unit * P : (unit + 1) * P, cols], in_=result[:, cols])
 
         def tile_starting_at(slot):
             i, j = divmod(slot, QUARTERS)
@@ -423,9 +435,9 @@ def tile_pairinteractiongrid_pa_kernel(tc, p, v, W1, b1, W2, b2, out):
             i, u = divmod(unit, QUARTERS)
             layer2_slot = unit + LAYER2_LAG
             if i == LAST - 2:
-                layer2_slot = unit + 6
+                layer2_slot = L5[u]
             elif i == LAST - 1:
-                layer2_slot = UNITS - 3 + (u + 1) // 2
+                layer2_slot = L6[u]
             elif i == LAST:
                 layer2_slot = LL[u]
             layer2_slices.setdefault(layer2_slot, []).append(unit)
@@ -497,9 +509,12 @@ def tile_pairinteractiongrid_pa_kernel(tc, p, v, W1, b1, W2, b2, out):
                 quantise_weight(slot + 1)
             i, u = divmod(slot - HIDDEN_LAG, QUARTERS)
             if LAST - 2 <= i < LAST:
-                if u == 0:
-                    regroup_hidden_shared(i, 0, TILE_ROWS)
-                elif u == 1:
+                if u == RU[i - LAST + 2]:
+                    cut = SH[i - LAST + 2]
+                    if cut > 0:
+                        regroup_hidden(i, nc.vector.tensor_copy, 0, cut)
+                    regroup_hidden(i, nc.scalar.copy, cut, TILE_ROWS - cut)
+                if u == QU[i - LAST + 2]:
                     quantise_hidden(i, 0, TILE_ROWS)
             elif 0 <= i < LAST - 2:
                 if u == 0 and HV[i] > 0:
@@ -522,4 +537,6 @@ def tile_pairinteractiongrid_pa_kernel(tc, p, v, W1, b1, W2, b2, out):
             for unit in layer2_slices.get(slot, []):
                 layer2_slice(unit)
             if slot == PBS:
-                make_p_bias()
+                make_p_bias(1)
+                if 5 in HB or 4 in HB:
+                    make_p_bias(0)

@@ -39,7 +39,7 @@ VD = (0, 0, 0, 2, 2, 2, 2, 2)
 WSC = ((1, 3), (1, 3), (1, 3), (1, 3), (1,))
 HV = (4, 1, 1, 1, 1, 1, 1, 1)
 DQ = 2
-EARLY_PIECES = 1
+EARLY_PIECES = 2
 BLOCKS = ((0, 256), (256, 128), (384, 128))
 WORK = {28: [(0, 0), (0, 1)], 29: [(0, 2), (0, 3)], 30: [(1, 0), (1, 1), (1, 2), (1, 3)], 31: [(2, 0), (2, 1), (2, 2), (2, 3)]}
 REG = {30: 0, 31: 1, 32: 2}
@@ -91,20 +91,28 @@ def tile_pairinteractiongrid_pa_kernel(tc, p, v, W1, b1, W2, b2, out):
         nc.gpsimd.memset(b1_rows[:], 0.0)
         nc.gpsimd.memset(odd_inputs_by_row[:].bitcast(F32), 0.0)
         load_inputs(0)
-        weight_raw = []
-        for c in range(PARTS + 1):
-            if c == 2:
-                nc.sync.dma_start(out=b1_rows[0:PACK, :], in_=b1.rearrange("(t q) -> t q", q=P))
-            if c == PARTS:
-                load_odd_inputs(0)
-                load_inputs(1)
+        weight_raw = {}
+
+        def load_weights(c):
             rows = W2 if c == PARTS else W1[c * K_PASS : (c + 1) * K_PASS, :]
             raw = weights.tile([P, PACK, F], BF16, bufs=PARTS + 1)
             nc.sync.dma_start(out=raw[:], in_=rows.rearrange("(t q) f -> q t f", q=P))
-            weight_raw.append(raw)
-        load_odd_inputs(1)
+            weight_raw[c] = raw
+
         b2_everywhere = consts.tile([P, D], BF16)
-        nc.sync.dma_start(out=b2_everywhere[:], in_=b2.partition_broadcast(P))
+
+        def load_rest():
+            load_odd_inputs(0)
+            load_inputs(1)
+            load_weights(PARTS)
+            load_odd_inputs(1)
+            nc.sync.dma_start(out=b2_everywhere[:], in_=b2.partition_broadcast(P))
+
+        load_weights(0)
+        load_weights(1)
+        nc.sync.dma_start(out=b1_rows[0:PACK, :], in_=b1.rearrange("(t q) -> t q", q=P))
+        load_weights(2)
+        load_weights(3)
 
         zero_column = consts.tile([P, 1], F32)
         nc.vector.memset(zero_column[:], 0.0)
@@ -128,13 +136,12 @@ def tile_pairinteractiongrid_pa_kernel(tc, p, v, W1, b1, W2, b2, out):
 
         by_k = consts.tile([P, 2, P, PACK], BF16, align_bytes=64)
 
-        def transpose_inputs(h, copy_v):
+        def transpose_inputs(h):
             transposed = psum.tile([P, PACK, P], BF16, tag="layer1", bufs=4)
             for t in range(PACK):
                 nc.tensor.transpose(transposed[:, t, :], inputs_by_row[:, h, t * P : (t + 1) * P], identity[:])
             by_row = transposed[:].rearrange("q t r -> q r t")
-            nc.scalar.copy(out=by_k[:, h, 0:64, :], in_=by_row[:, 0:64, :])
-            copy_v(out=by_k[:, h, 64:128, :], in_=by_row[:, 64:128, :])
+            nc.scalar.copy(out=by_k[:, h, :, :], in_=by_row)
 
         b1_by_group = consts.tile([P, QUARTERS], F32)
 
@@ -293,7 +300,8 @@ def tile_pairinteractiongrid_pa_kernel(tc, p, v, W1, b1, W2, b2, out):
                 in_=p_scales[:, h, first : first + 4 * TILE_POINTS].bitcast(I32).unsqueeze(2).to_broadcast([P, TILE_POINTS, 8]),
             )
             p_part[i] = (codes, scales)
-            spread_v(i, h, e)
+            if i > 0:
+                spread_v(i, h, e)
 
         def spread_v(i, h, e):
             if i % 2 == 1:
@@ -301,12 +309,11 @@ def tile_pairinteractiongrid_pa_kernel(tc, p, v, W1, b1, W2, b2, out):
                 return
             codes = pairs.tile([P, TILE_ROWS], U32, align_bytes=256, name="v_part_codes")
             scales = pairs.tile([P, TILE_ROWS], U8, align_bytes=256, name="v_part_scales")
-            move = nc.vector.tensor_copy if i == 0 else nc.sync.dma_start
-            move(
+            nc.sync.dma_start(
                 out=codes[:].bitcast(I32).rearrange("q (n m) -> q n m", m=POINTS),
                 in_=v_codes[:, h, POINTS * e : POINTS * (e + 1)].bitcast(I32).unsqueeze(1).to_broadcast([P, TILE_POINTS, POINTS]),
             )
-            move(
+            nc.sync.dma_start(
                 out=scales[:].bitcast(I32).rearrange("q (n c) -> q n c", c=POINTS // 4),
                 in_=v_scales[:, h, POINTS * e : POINTS * (e + 1)].bitcast(I32).unsqueeze(1).to_broadcast([P, TILE_POINTS, POINTS // 4]),
             )
@@ -458,9 +465,11 @@ def tile_pairinteractiongrid_pa_kernel(tc, p, v, W1, b1, W2, b2, out):
 
         for w in range(EARLY_PIECES):
             regroup_weight(w, (0,))
-        transpose_inputs(0, nc.vector.tensor_copy)
+        transpose_inputs(0)
         repeat_p(0)
         quantise_v(0)
+        spread_v(0, 0, 0)
+        load_rest()
         multiply(0)
         quantise_p(0)
         difference_slice(0)
@@ -477,7 +486,7 @@ def tile_pairinteractiongrid_pa_kernel(tc, p, v, W1, b1, W2, b2, out):
 
         for slot in range(UNITS + 2):
             if slot == INPUT_SLOT:
-                transpose_inputs(1, nc.scalar.copy)
+                transpose_inputs(1)
             if slot == INPUT_SLOT + 2:
                 repeat_p(1)
                 quantise_v(1)

@@ -39,16 +39,16 @@ VD = (0, 0, 0, 2, 2, 2, 2, 2)
 WSC = ((1, 3), (1, 3), (1, 3), (1, 3), (1,))
 HV = (4, 1, 1, 1, 1, 1, 1, 1)
 DQ = 2
-EARLY_PIECES = 2
+EARLY_PIECES = 3
 BLOCKS = ((0, 256), (256, 128), (384, 128))
 WORK = {28: [(0, 0), (0, 1)], 29: [(0, 2), (0, 3)], 30: [(1, 0), (1, 1), (1, 2), (1, 3)], 31: [(2, 0), (2, 1), (2, 2), (2, 3)]}
 REG = {30: 0, 31: 1, 32: 2}
-LL = (31, 31, 32, 32)
+LL = (32, 32, 32, 32)
 SH = (384, 384)
-TD = 28
+TD = 20
 RU = (0, 0)
 QU = (1, 1)
-L5 = (26, 27, 28, 29)
+L5 = (27, 28, 29, 29)
 L6 = (29, 30, 30, 31)
 SPL = 2
 PBS = 22
@@ -93,11 +93,13 @@ def tile_pairinteractiongrid_pa_kernel(tc, p, v, W1, b1, W2, b2, out):
         load_inputs(0)
         weight_raw = {}
 
-        def load_weights(c):
+        def load_weights(c, first=0, columns=F):
             rows = W2 if c == PARTS else W1[c * K_PASS : (c + 1) * K_PASS, :]
-            raw = weights.tile([P, PACK, F], BF16, bufs=PARTS + 1)
-            nc.sync.dma_start(out=raw[:], in_=rows.rearrange("(t q) f -> q t f", q=P))
-            weight_raw[c] = raw
+            if c not in weight_raw:
+                raw = weights.tile([P, PACK, F], BF16, bufs=PARTS + 1)
+                weight_raw[c] = raw
+            cols = slice(first, first + columns)
+            nc.sync.dma_start(out=weight_raw[c][:, :, cols], in_=rows[:, cols].rearrange("(t q) f -> q t f", q=P))
 
         b2_everywhere = consts.tile([P, D], BF16)
 
@@ -493,7 +495,7 @@ def tile_pairinteractiongrid_pa_kernel(tc, p, v, W1, b1, W2, b2, out):
             if slot == INPUT_SLOT + 3:
                 quantise_p(1)
             if slot < W2_PIECE:
-                regroup_weight(slot + 1, (1, 2, 3) if slot + 1 < EARLY_PIECES else (0, 1, 2, 3))
+                regroup_weight(slot + 1, [c for c in range(4) if not (c == 0 and slot + 1 < EARLY_PIECES)])
 
             for unit in difference_slices.get(slot, []):
                 difference_slice(unit)

from contextlib import ExitStack

import concourse.mybir as mybir
from concourse.masks import make_identity

BF16 = mybir.dt.bfloat16
F32 = mybir.dt.float32
I32 = mybir.dt.int32
U32 = mybir.dt.uint32
U8 = mybir.dt.uint8
FP8X4 = mybir.dt.float8_e4m3fn_x4
ACT = mybir.ActivationFunctionType
ALU = mybir.AluOpType

P = 128
PACK = 4
K_PASS = P * PACK
STEPS = 4
POINTS = 32
D = 512
F = 512
TILE_ROWS = 512
TILE_POINTS = TILE_ROWS // POINTS
TILES = STEPS * POINTS * POINTS // TILE_ROWS
QUARTERS = 4
UNITS = TILES * QUARTERS
PARTS = 4
W2_PIECE = 4

INPUT_SLOT = 6
DIFFERENCE_LEAD = 7
PRODUCT_LEAD = 6
HIDDEN_LAG = 4
LAYER2_LAG = 8

HALF_ROWS = TILE_ROWS // 2
LAST = TILES - 1
VD = (0, 0, 0, 2, 2, 2, 2, 2)
WSC = ((1, 3), (1, 3), (1, 3), (1, 3), (1,))
HV = (4, 1, 1, 1, 1, 1, 1, 1)
DQ = 2
EARLY_PIECES = 3
BLOCKS = ((0, 256), (256, 128), (384, 128))
WORK = {28: [(0, 0), (0, 1)], 29: [(0, 2), (0, 3)], 30: [(1, 0), (1, 1), (1, 2), (1, 3)], 31: [(2, 0), (2, 1), (2, 2), (2, 3)]}
REG = {30: 0, 31: 1, 32: 2}
LL = (32, 32, 32, 32)
SH = (384, 384)
TD = 20
RU = (0, 0)
QU = (1, 1)
L5 = (27, 28, 29, 29)
L6 = (29, 30, 30, 31)
SPL = 2
PBS = 22
HB = (6, 7)
AH = {2: (1, 0)}

FLOPS = 2 * STEPS * POINTS * POINTS * (4 * D * F + F * D)


def tile_pairinteractiongrid_pa_kernel(tc, p, v, W1, b1, W2, b2, out):
    nc = tc.nc
    p_rows = p.flatten_outer_dims()
    v_rows = v.flatten_outer_dims()
    out_rows = out.flatten_outer_dims()

    with ExitStack() as stack:
        consts = stack.enter_context(tc.tile_pool(name="consts", bufs=1))
        weights = stack.enter_context(tc.tile_pool(name="weights", bufs=3))
        pairs = stack.enter_context(tc.tile_pool(name="pairs", bufs=2))
        hidden = stack.enter_context(tc.tile_pool(name="hidden", bufs=2))
        results = stack.enter_context(tc.tile_pool(name="results", bufs=6))
        psum = stack.enter_context(tc.psum_pool(name="psum", bufs=2))
        stack.enter_context(tc.manual_schedule())

        inputs_by_row = consts.tile([P, 2, D], BF16)
        odd_inputs_by_row = consts.tile([P, 2, D], BF16)

        def load_inputs(h):
            nc.sync.dma_start(out=inputs_by_row[0:64, h, :], in_=p_rows[64 * h : 64 * (h + 1), :])
            nc.sync.dma_start(out=inputs_by_row[64:128, h, :], in_=v_rows[64 * h : 64 * (h + 1), :])

        def load_odd_inputs(h):
            odd_rows = slice(64 * h + POINTS, 64 * (h + 1))
            nc.sync.dma_start(out=odd_inputs_by_row[0:POINTS, h, :], in_=p_rows[odd_rows, :])
            nc.sync.dma_start(out=odd_inputs_by_row[64 : 64 + POINTS, h, :], in_=v_rows[odd_rows, :])

        b1_rows = consts.tile([P, P], BF16)
        identity = consts.tile([P, P], BF16)
        make_identity(nc, identity[:])
        nc.gpsimd.memset(b1_rows[:], 0.0)
        nc.gpsimd.memset(odd_inputs_by_row[:].bitcast(F32), 0.0)
        load_inputs(0)
        weight_raw = {}

        def load_weights(c, first=0, columns=F):
            rows = W2 if c == PARTS else W1[c * K_PASS : (c + 1) * K_PASS, :]
            if c not in weight_raw:
                raw = weights.tile([P, PACK, F], BF16, bufs=PARTS + 1)
                weight_raw[c] = raw
            cols = slice(first, first + columns)
            nc.sync.dma_start(out=weight_raw[c][:, :, cols], in_=rows[:, cols].rearrange("(t q) f -> q t f", q=P))

        b2_everywhere = consts.tile([P, D], BF16)

        def load_rest():
            load_odd_inputs(0)
            load_inputs(1)
            load_weights(PARTS)
            load_odd_inputs(1)
            nc.sync.dma_start(out=b2_everywhere[:], in_=b2.partition_broadcast(P))

        load_weights(0)
        load_weights(1)
        nc.sync.dma_start(out=b1_rows[0:PACK, :], in_=b1.rearrange("(t q) -> t q", q=P))
        load_weights(2)
        load_weights(3)

        zero_column = consts.tile([P, 1], F32)
        nc.vector.memset(zero_column[:], 0.0)
        warm_column = consts.tile([P, 1], F32)
        nc.scalar.activation(out=warm_column[:], in_=zero_column[:], func=ACT.Silu)

        p_codes = consts.tile([P, 2, 64 * 4], U32, align_bytes=256)
        p_scales = consts.tile([P, 2, 64 * 4], U8, align_bytes=256)
        v_codes = consts.tile([P, 2, 64], U32, align_bytes=256)
        v_scales = consts.tile([P, 2, 64], U8, align_bytes=256)
        nc.vector.memset(p_scales[:].bitcast(I32), 0)
        nc.vector.memset(v_scales[:].bitcast(I32), 0)

        chooser = consts.tile([P, POINTS, POINTS], BF16)
        nc.vector.tensor_tensor(
            out=chooser[:],
            in0=identity[:, 0:POINTS].unsqueeze(2).to_broadcast([P, POINTS, POINTS]),
            in1=identity[:, 64 : 64 + POINTS].unsqueeze(1).to_broadcast([P, POINTS, POINTS]),
            op=ALU.subtract,
        )

        by_k = consts.tile([P, 2, P, PACK], BF16, align_bytes=64)

        def transpose_inputs(h):
            transposed = psum.tile([P, PACK, P], BF16, tag="layer1", bufs=4)
            for t in range(PACK):
                nc.tensor.transpose(transposed[:, t, :], inputs_by_row[:, h, t * P : (t + 1) * P], identity[:])
            by_row = transposed[:].rearrange("q t r -> q r t")
            nc.scalar.copy(out=by_k[:, h, :, :], in_=by_row)

        b1_by_group = consts.tile([P, QUARTERS], F32)

        def transpose_b1():
            b1_transposed = psum.tile([P, P], BF16, tag="layer2")
            nc.tensor.transpose(b1_transposed[:], b1_rows[:], identity[:])
            nc.vector.tensor_copy(out=b1_by_group[:], in_=b1_transposed[:, 0:QUARTERS])

        p_fourfold = {}

        def repeat_p(h):
            fourfold = pairs.tile([P, 64, 4, PACK], BF16, align_bytes=64)
            nc.vector.tensor_copy(
                out=fourfold[:], in_=by_k[:, h, 0:64, :].unsqueeze(2).to_broadcast([P, 64, 4, PACK])
            )
            p_fourfold[h] = fourfold

        def quantise_v(h):
            nc.vector.quantize_mx(
                out=v_codes[:, h, :].bitcast(FP8X4),
                scales=v_scales[:, h, :],
                in_=by_k[:, h, 64:128, :].rearrange("q r t -> q (r t)"),
            )

        def quantise_p(h):
            nc.vector.quantize_mx(
                out=p_codes[:, h, :].bitcast(FP8X4),
                scales=p_scales[:, h, :],
                in_=p_fourfold[h][:].rearrange("q r c t -> q (r c t)"),
            )

        weight_codes = consts.tile([P, W2_PIECE + 1, F], U32, align_bytes=256)
        weight_scales = consts.tile([P, W2_PIECE + 1, F], U8, align_bytes=256)
        weight_grouped = {}

        def regroup(copy, grouped, planes):
            copy(
                out=grouped.rearrange("q (c i) t -> q c t i", i=4),
                in_=planes.rearrange("q t (c i) -> q c t i", i=4),
            )

        def regroup_weight(w, cs=(0, 1, 2, 3)):
            if w not in weight_grouped:
                grouped = weights.tile([P, PARTS, P, PACK], BF16, align_bytes=64)
                weight_grouped[w] = grouped
            for c in cs:
                if w == W2_PIECE:
                    block = weight_raw[PARTS][:, :, c * P : (c + 1) * P]
                else:
                    block = weight_raw[c][:, :, w * P : (w + 1) * P]
                regroup(nc.scalar.copy if c in WSC[w] else nc.vector.tensor_copy, weight_grouped[w][:, c, :, :], block)

        def quantise_weight(w):
            nc.vector.quantize_mx(
                out=weight_codes[:, w, :].bitcast(FP8X4),
                scales=weight_scales[:, w, :],
                in_=weight_grouped[w][:].rearrange("q c f t -> q (c f t)"),
            )

        p_part = {}
        v_part = {}
        product_part = {}
        difference_part = {}
        product_values = {}
        difference_values = {}
        hidden_planes = {}
        signed_values = {}
        layer1_banks = {}
        hidden_grouped = {}
        hidden_part = {}
        layer2_banks = {}

        def difference_slice(unit):
            i, u = divmod(unit, QUARTERS)
            step, half = divmod(i, 2)
            h, e = divmod(step, 2)
            if u == 0:
                values = pairs.tile([P, TILE_ROWS, PACK], BF16, align_bytes=64, name="difference_values")
                difference_values[i] = values
            if u < VD[i]:
                if u == 0:
                    points = 4 * VD[i]
                    first_p = POINTS * e + TILE_POINTS * half
                    first_v = 64 + POINTS * e
                    shape = [P, points, POINTS, PACK]
                    signed = pairs.tile([P, TILE_POINTS, POINTS, PACK], BF16, align_bytes=64)
                    nc.vector.tensor_tensor(
                        out=signed[:, 0:points, :, :],
                        in0=by_k[:, h, first_p : first_p + points, :].unsqueeze(2).to_broadcast(shape),
                        in1=by_k[:, h, first_v : first_v + POINTS, :].unsqueeze(1).to_broadcast(shape),
                        op=ALU.subtract,
                    )
                    signed_values[i] = signed
                if u == VD[i] - 1:
                    nc.scalar.activation(
                        out=difference_values[i][:, 0 : VD[i] * P, :],
                        in_=signed_values[i][:, 0 : 4 * VD[i], :, :].rearrange("q n m t -> q (n m) t"),
                        func=ACT.Abs,
                    )
                return
            first_point = TILE_POINTS * half + 4 * u
            rows = (odd_inputs_by_row if e else inputs_by_row)[:, h, :]
            bank = psum.tile([P, PACK, P], F32, tag="difference")
            for t in range(PACK):
                nc.tensor.matmul(
                    out=bank[:, t, :],
                    lhsT=rows[:, t * P : (t + 1) * P],
                    rhs=chooser[:, first_point : first_point + 4, :].rearrange("k n m -> k (n m)"),
                    start=True,
                    stop=True,
                )
            nc.scalar.activation(
                out=difference_values[i][:, u * P : (u + 1) * P, :],
                in_=bank[:].rearrange("q t r -> q r t"),
                func=ACT.Abs,
            )

        def quantise(values, name):
            codes = pairs.tile([P, TILE_ROWS], U32, align_bytes=256, name=name + "_codes", bufs=3)
            scales = pairs.tile([P, TILE_ROWS], U8, align_bytes=256, name=name + "_scales", bufs=3)
            nc.vector.quantize_mx(out=codes[:].bitcast(FP8X4), scales=scales[:], in_=values)
            return codes, scales

        def multiply(i):
            h, e = divmod(i // 2, 2)
            first_p = TILE_POINTS * (i % 4)
            first_v = 64 + POINTS * e
            values = pairs.tile([P, TILE_POINTS, POINTS, PACK], BF16, align_bytes=64, name="product_values")
            shape = [P, TILE_POINTS, POINTS, PACK]
            nc.vector.tensor_tensor(
                out=values[:],
                in0=by_k[:, h, first_p : first_p + TILE_POINTS, :].unsqueeze(2).to_broadcast(shape),
                in1=by_k[:, h, first_v : first_v + POINTS, :].unsqueeze(1).to_broadcast(shape),
                op=ALU.mult,
            )
            product_values[i] = values

        def spread_p_and_v(i):
            h, e = divmod(i // 2, 2)
            if i in HB:
                spread_v(i, h, e)
                return
            codes = pairs.tile([P, TILE_ROWS], U32, align_bytes=256, name="p_part_codes", bufs=3)
            scales = pairs.tile([P, TILE_ROWS], U8, align_bytes=256, name="p_part_scales", bufs=3)
            first = 4 * TILE_POINTS * (i % 4)
            nc.vector.tensor_copy(
                out=codes[:].bitcast(I32).rearrange("q (n r c) -> q n r c", r=8, c=4),
                in_=p_codes[:, h, first : first + 4 * TILE_POINTS]
                .bitcast(I32)
                .rearrange("q (n c) -> q n c", c=4)
                .unsqueeze(2)
                .to_broadcast([P, TILE_POINTS, 8, 4]),
            )
            nc.vector.tensor_copy(
                out=scales[:].bitcast(I32).rearrange("q (n r) -> q n r", r=8),
                in_=p_scales[:, h, first : first + 4 * TILE_POINTS].bitcast(I32).unsqueeze(2).to_broadcast([P, TILE_POINTS, 8]),
            )
            p_part[i] = (codes, scales)
            if i > 0:
                spread_v(i, h, e)

        def spread_v(i, h, e):
            if i % 2 == 1:
                v_part[i] = v_part[i - 1]
                return
            codes = pairs.tile([P, TILE_ROWS], U32, align_bytes=256, name="v_part_codes")
            scales = pairs.tile([P, TILE_ROWS], U8, align_bytes=256, name="v_part_scales")
            nc.sync.dma_start(
                out=codes[:].bitcast(I32).rearrange("q (n m) -> q n m", m=POINTS),
                in_=v_codes[:, h, POINTS * e : POINTS * (e + 1)].bitcast(I32).unsqueeze(1).to_broadcast([P, TILE_POINTS, POINTS]),
            )
            nc.sync.dma_start(
                out=scales[:].bitcast(I32).rearrange("q (n c) -> q n c", c=POINTS // 4),
                in_=v_scales[:, h, POINTS * e : POINTS * (e + 1)].bitcast(I32).unsqueeze(1).to_broadcast([P, TILE_POINTS, POINTS // 4]),
            )
            v_part[i] = (codes, scales)

        p_bias = consts.tile([P, QUARTERS, 2 * POINTS], F32)

        def make_p_bias(e):
            bank = psum.tile([P, QUARTERS, P], F32, tag="difference")
            for j in range(QUARTERS):
                nc.tensor.matmul_mx(
                    out=bank[:, j, :],
                    lhsT=weight_codes[:, j, 0:P].bitcast(FP8X4),
                    lhsT_scale=weight_scales[:, j, 0:P],
                    rhs=p_codes[:, 1, P * e : P * (e + 1)].bitcast(FP8X4),
                    rhs_scale=p_scales[:, 1, P * e : P * (e + 1)],
                    start=True,
                    stop=True,
                )
            for j in range(QUARTERS):
                nc.scalar.activation(
                    out=p_bias[:, j, POINTS * e : POINTS * (e + 1)],
                    in_=bank[:, j, :].rearrange("q (n c) -> q n c", c=4)[:, :, 0],
                    func=ACT.Identity,
                    bias=b1_by_group[:, j : j + 1],
                )

        def layer1_passes(i, j, first, rows, cs):
            if (i, j, first) not in layer1_banks:
                bank = psum.tile([P, TILE_ROWS], F32, tag="layer1", bufs=4)
                layer1_banks[i, j, first] = bank
            bank = layer1_banks[i, j, first]
            for c in cs:
                if c == 0 and i in HB:
                    continue
                codes, scales = [p_part, v_part, product_part, difference_part][c][i]
                nc.tensor.matmul_mx(
                    out=bank[:, 0:rows],
                    lhsT=weight_codes[:, j, c * P : (c + 1) * P].bitcast(FP8X4),
                    lhsT_scale=weight_scales[:, j, c * P : (c + 1) * P],
                    rhs=codes[:, first : first + rows].bitcast(FP8X4),
                    rhs_scale=scales[:, first : first + rows],
                    start=(c == (1 if i in HB else 0)),
                    stop=(c == PARTS - 1),
                )

        def layer1_group(i, j, first, rows):
            if j == 0 and first == 0:
                planes = hidden.tile([P, QUARTERS, TILE_ROWS], BF16, name="hidden_planes")
                hidden_planes[i] = planes
            if (i, j, first) not in layer1_banks:
                layer1_passes(i, j, first, rows, (0, 1))
            layer1_passes(i, j, first, rows, (2, 3))
            bank = layer1_banks[i, j, first]
            if i in HB:
                point = TILE_POINTS * (i % 4) + first // POINTS
                for n in range(rows // POINTS):
                    nc.scalar.activation(
                        out=hidden_planes[i][:, j, first + n * POINTS : first + (n + 1) * POINTS],
                        in_=bank[:, n * POINTS : (n + 1) * POINTS],
                        func=ACT.Silu,
                        bias=p_bias[:, j, point + n : point + n + 1],
                    )
            else:
                nc.scalar.activation(
                    out=hidden_planes[i][:, j, first : first + rows],
                    in_=bank[:, 0:rows],
                    func=ACT.Silu,
                    bias=b1_by_group[:, j : j + 1],
                )

        def regroup_hidden(i, copy, first, rows):
            if i not in hidden_grouped:
                grouped = hidden.tile([P, TILE_ROWS, PACK], BF16, align_bytes=64, name="hidden_grouped")
                hidden_grouped[i] = grouped
            end = first + rows
            regroup(copy, hidden_grouped[i][:, first:end, :], hidden_planes[i][:, :, first:end])

        def regroup_hidden_shared(i, first, rows):
            regroup_hidden(i, nc.vector.tensor_copy, first, rows // 2)
            regroup_hidden(i, nc.scalar.copy, first + rows // 2, rows // 2)

        def quantise_hidden(i, first, rows):
            if first == 0:
                codes = hidden.tile([P, TILE_ROWS], U32, align_bytes=256, name="hidden_codes")
                scales = hidden.tile([P, TILE_ROWS], U8, align_bytes=256, name="hidden_scales")
                hidden_part[i] = (codes, scales)
            codes, scales = hidden_part[i]
            nc.vector.quantize_mx(
                out=codes[:, first : first + rows].bitcast(FP8X4),
                scales=scales[:, first : first + rows],
                in_=hidden_grouped[i][:, first : first + rows, :].rearrange("q r t -> q (r t)"),
            )

        def layer2_slice(unit):
            i, u = divmod(unit, QUARTERS)
            codes, scales = hidden_part[i]
            bank = psum.tile([P, D], F32, tag="difference" if unit >= TD and unit % 2 else "layer2", name="bank")
            nc.tensor.matmul_mx(
                out=bank[:],
                lhsT=codes[:, u * P : (u + 1) * P].bitcast(FP8X4),
                lhsT_scale=scales[:, u * P : (u + 1) * P],
                rhs=weight_codes[:, W2_PIECE, :].bitcast(FP8X4),
                rhs_scale=weight_scales[:, W2_PIECE, :],
                start=True,
                stop=True,
            )
            layer2_banks[unit] = bank

        def add_bias_and_store(unit):
            result = results.tile([P, D], F32)
            width = D // (SPL if unit == UNITS - 1 else 1)
            for a in range(0, D, width):
                cols = slice(a, a + width)
                nc.vector.tensor_tensor(
                    out=result[:, cols], in0=layer2_banks[unit][:, cols], in1=b2_everywhere[:, cols], op=ALU.add
                )
                nc.sync.dma_start(out=out_rows[unit * P : (unit + 1) * P, cols], in_=result[:, cols])

        def tile_starting_at(slot):
            i, j = divmod(slot, QUARTERS)
            return i if j == 0 and 0 <= i < TILES else None

        layer2_slices = {}
        for unit in range(UNITS):
            i, u = divmod(unit, QUARTERS)
            layer2_slot = unit + LAYER2_LAG
            if i == LAST - 2:
                layer2_slot = L5[u]
            elif i == LAST - 1:
                layer2_slot = L6[u]
            elif i == LAST:
                layer2_slot = LL[u]
            layer2_slices.setdefault(layer2_slot, []).append(unit)

        difference_slices = {}
        for unit in range(QUARTERS, UNITS):
            slot = max(unit - DIFFERENCE_LEAD, (unit - QUARTERS) // 2)
            difference_slices.setdefault(slot, []).append(unit)
        multiply_slots = {max(QUARTERS * i - PRODUCT_LEAD, 0): i for i in range(1, TILES)}
        product_slots = {max(QUARTERS * i - PRODUCT_LEAD + 1, 1): i for i in range(1, TILES)}
        difference_slots = {max(QUARTERS * i - DQ, 2): i for i in range(1, TILES)}

        def quantise_product(i):
            product_part[i] = quantise(product_values[i][:].rearrange("q n m t -> q (n m t)"), "product")

        def quantise_difference(i):
            difference_part[i] = quantise(difference_values[i][:].rearrange("q r t -> q (r t)"), "difference")

        for w in range(EARLY_PIECES):
            regroup_weight(w, (0,))
        transpose_inputs(0)
        repeat_p(0)
        quantise_v(0)
        spread_v(0, 0, 0)
        load_rest()
        multiply(0)
        quantise_p(0)
        difference_slice(0)
        difference_slice(1)
        regroup_weight(0, (1, 2))
        difference_slice(2)
        difference_slice(3)
        regroup_weight(0, (3,))
        quantise_product(0)
        spread_p_and_v(0)
        transpose_b1()
        quantise_weight(0)
        quantise_difference(0)

        for slot in range(UNITS + 2):
            if slot == INPUT_SLOT:
                transpose_inputs(1)
            if slot == INPUT_SLOT + 2:
                repeat_p(1)
                quantise_v(1)
            if slot == INPUT_SLOT + 3:
                quantise_p(1)
            if slot < W2_PIECE:
                regroup_weight(slot + 1, [c for c in range(4) if not (c == 0 and slot + 1 < EARLY_PIECES)])

            for unit in difference_slices.get(slot, []):
                difference_slice(unit)
            if slot in multiply_slots:
                multiply(multiply_slots[slot])
            stored = layer2_slices.get(slot - 1, [])
            last_block = BLOCKS[REG[slot]] if slot in REG else None
            for unit in stored[:-1]:
                add_bias_and_store(unit)
            if last_block is not None:
                regroup_hidden_shared(LAST, *last_block)
            for unit in stored[-1:]:
                add_bias_and_store(unit)
            if last_block is not None:
                quantise_hidden(LAST, *last_block)
            if slot in product_slots:
                spread_p_and_v(product_slots[slot])
                quantise_product(product_slots[slot])
            if slot in difference_slots:
                quantise_difference(difference_slots[slot])
            if slot < W2_PIECE:
                quantise_weight(slot + 1)
            i, u = divmod(slot - HIDDEN_LAG, QUARTERS)
            if LAST - 2 <= i < LAST:
                if u == RU[i - LAST + 2]:
                    cut = SH[i - LAST + 2]
                    if cut > 0:
                        regroup_hidden(i, nc.vector.tensor_copy, 0, cut)
                    regroup_hidden(i, nc.scalar.copy, cut, TILE_ROWS - cut)
                if u == QU[i - LAST + 2]:
                    quantise_hidden(i, 0, TILE_ROWS)
            elif 0 <= i < LAST - 2:
                if u == 0 and HV[i] > 0:
                    regroup_hidden(i, nc.vector.tensor_copy, 0, P * HV[i])
                for s in range(HV[i], QUARTERS):
                    if max(s - 1, 0) == u:
                        regroup_hidden(i, nc.scalar.copy, s * P, P)
                if u == 3:
                    quantise_hidden(i, 0, TILE_ROWS)

            if 0 <= slot < UNITS:
                i, j = divmod(slot, QUARTERS)
                if slot in AH:
                    layer1_passes(*AH[slot], 0, TILE_ROWS, (0, 1))
                if i != LAST:
                    layer1_group(i, j, 0, TILE_ROWS)
                else:
                    for b, group in WORK[slot]:
                        layer1_group(i, group, *BLOCKS[b])
            for unit in layer2_slices.get(slot, []):
                layer2_slice(unit)
            if slot == PBS:
                make_p_bias(1)
                if 5 in HB or 4 in HB:
                    make_p_bias(0)
